import numpy as np
import ml_dtypes


def mxq(x, axis, fmt="e4m3"):
    dtype, down = {"e4m3": (ml_dtypes.float8_e4m3fn, 7), "e5m2": (ml_dtypes.float8_e5m2, 14)}[fmt]
    v = np.moveaxis(np.asarray(x, np.float32).astype(ml_dtypes.bfloat16).astype(np.float64), axis, -1)
    blocks = v.reshape(v.shape[:-1] + (-1, 32))
    amax = np.abs(blocks).max(-1, keepdims=True)
    byte = np.maximum(np.where(amax > 0, np.frexp(amax)[1] - 1 + 127, 0) - down, 1)
    scale = np.exp2(byte - 127.0)
    codes = (blocks / scale).astype(np.float32).astype(dtype).astype(np.float64)
    return np.moveaxis((codes * scale).reshape(v.shape), -1, axis)


WIDE = False


def mx_kscale(k):
    if not WIDE:
        return np.ones(k)
    levels = np.array([10, -10, 5, -5, 0])
    a = np.random.permutation(np.resize(levels, k // 512 * 4)).reshape(k // 512, 4)
    idx = np.arange(k)
    return np.exp2(a[idx // 512, idx % 128 // 32])


BF16 = ml_dtypes.bfloat16


def bf(x):
    return np.asarray(x, np.float32).astype(BF16)


def f64(x):
    return np.asarray(x).astype(np.float64)


E2M1 = np.array([0.0, 0.5, 1.0, 1.5, 2.0, 3.0, 4.0, 6.0, -0.0, -0.5, -1.0, -1.5, -2.0, -3.0, -4.0, -6.0])


def pack_weight(w, fmt):
    k, n = w.shape
    w = f64(bf(w)).reshape(k // 32, 32, n)
    amax = np.abs(w).max(1)
    if fmt == "e4m3":
        byte = np.frexp(amax)[1] - 1 + 127 - 7
    else:
        mant, ex = np.frexp(amax / 6.0)
        byte = np.where(mant > 0.5, ex, ex - 1) + 127
    byte = np.clip(np.where(amax > 0, byte, 1), 1, 254)
    scaled = (w * np.exp2(127.0 - byte)[:, None, :]).reshape(k, n).astype(np.float32)
    by_word = np.ascontiguousarray(scaled.reshape(k // 512, 128, 4, n).transpose(0, 1, 3, 2))
    if fmt == "e4m3":
        words = by_word.astype(ml_dtypes.float8_e4m3fn).view(np.uint8)
    else:
        c = by_word.astype(ml_dtypes.float4_e2m1fn).view(np.uint8) & 0xF
        words = c[..., 0::2] | (c[..., 1::2] << 4)
    return np.ascontiguousarray(words), np.ascontiguousarray(byte.astype(np.uint8).reshape(k // 512, 16, n))


def unpack_weight(words, scales, fmt):
    g, p, n, _ = words.shape
    if fmt == "e4m3":
        vals = np.ascontiguousarray(words).view(ml_dtypes.float8_e4m3fn).astype(np.float64)
    else:
        nib = np.empty((g, p, n, 4), np.uint8)
        nib[..., 0::2] = words & 0xF
        nib[..., 1::2] = words >> 4
        vals = E2M1[nib]
    vals = vals * np.repeat(np.exp2(scales.astype(np.float64) - 127.0), 8, axis=1)[..., None]
    return vals.transpose(0, 1, 3, 2).reshape(g * 512, n)

def pack4(w):
    words, scales = pack_weight(w, "e2m1")
    return words.reshape(words.shape[0], 128, -1), scales


def unpack4(words, scales):
    return unpack_weight(words.reshape(words.shape[0], 128, -1, 2), scales, "e2m1")


B, D, F, A, M = 2048, 1024, 1024, 32, 512
G = 11.0


def setup_inputs():
    s = mx_kscale(D)
    r = 0.5 + np.random.random_sample((B, 1))
    next_state = bf(np.random.standard_normal((B, D)) * r * s)
    seen = bf(np.maximum(np.random.standard_normal((M, F)), 0.0) * G / np.sqrt(F))
    wf = np.random.standard_normal((F, D)) * G / np.sqrt(D * F) / s
    words, scales = pack4(np.ascontiguousarray(wf.T))
    b_feat = bf(np.random.standard_normal(F) * 0.5 * G / np.sqrt(F))
    return {"next_state": next_state,
            "seen": seen,
            "Wf_words": words,
            "Wf_scales": scales,
            "b_feat": b_feat}


def reference(next_state, seen, Wf_words, Wf_scales, b_feat):
    mem = f64(seen)
    fa = np.maximum((mxq(f64(next_state), 1, "e4m3") @ unpack4(Wf_words, Wf_scales)) + f64(b_feat), 0.0)
    a2 = np.sum(fa ** 2, axis=-1, keepdims=True)
    s2 = np.sum(mem ** 2, axis=-1)
    d2 = a2 + s2[None, :] - 2.0 * (mxq(fa, 1, "e4m3") @ mxq(mem, 1, "e4m3").T)
    min_dist = np.sqrt(np.maximum(np.min(d2, axis=-1), 0.0))
    return np.minimum(1.0, min_dist / 10.0)

@@ -1,0 +1,281 @@
+from contextlib import ExitStack
+
+import concourse.mybir as mybir
+from concourse.masks import make_identity
+
+F32 = mybir.dt.float32
+BF16 = mybir.dt.bfloat16
+I32 = mybir.dt.int32
+U32 = mybir.dt.uint32
+U8 = mybir.dt.uint8
+FP8X4 = mybir.dt.float8_e4m3fn_x4
+FP4X4 = mybir.dt.float4_e2m1fn_x4
+ALU = mybir.AluOpType
+ACT = mybir.ActivationFunctionType
+AXIS_X = mybir.AxisListType.X
+
+P = 128
+PACK = 4
+K_PASS = P * PACK
+
+STATES = 2048
+STATE_DIM = 1024
+FEATURES = 1024
+MEMORY = 512
+
+IN_PASSES = STATE_DIM // K_PASS
+FEAT_PASSES = FEATURES // K_PASS
+FEAT_TILES = FEATURES // P
+MEM_TILES = MEMORY // P
+STATE_TILES = STATES // P
+CHUNK = 512
+CHUNK_TILES = CHUNK // P
+CHUNKS = STATES // CHUNK
+WORD_PLANES = 2
+AHEAD = 2
+SQRT_FLOOR = 1e-30
+
+FLOPS = 2 * STATES * STATE_DIM * FEATURES + 2 * STATES * FEATURES * MEMORY
+
+
+def tile_curiositymodule_pa_kernel(tc, next_state, seen, Wf_words, Wf_scales, b_feat, out):
+    nc = tc.nc
+    with ExitStack() as ctx:
+        keep = ctx.enter_context(tc.tile_pool(name="keep", bufs=1))
+        work = ctx.enter_context(tc.tile_pool(name="work", bufs=2))
+        psum_t = ctx.enter_context(tc.psum_pool(name="psum_t", bufs=4))
+        psum_mx = ctx.enter_context(tc.psum_pool(name="psum_mx", bufs=4))
+        ctx.enter_context(tc.manual_schedule())
+
+        x_sb = keep.tile([P, STATE_TILES, STATE_DIM], BF16)
+        seen_sb = keep.tile([P, MEM_TILES, FEATURES], BF16)
+        w_words = keep.tile([P, IN_PASSES, 2 * FEATURES], U8, align_bytes=64)
+        w_scales = keep.tile([P, IN_PASSES, FEATURES], U8, align_bytes=64)
+        x_codes = keep.tile([P, CHUNKS, IN_PASSES, CHUNK], U32, align_bytes=64)
+        x_scales = keep.tile([P, CHUNKS, IN_PASSES, CHUNK], U8, align_bytes=64)
+        seen_grouped = keep.tile([P, FEAT_PASSES, MEMORY * PACK], BF16, align_bytes=64)
+        seen_codes = keep.tile([P, FEAT_PASSES, MEMORY], U32, align_bytes=64)
+        seen_scales = keep.tile([P, FEAT_PASSES, MEMORY], U8, align_bytes=64)
+        ident_f32 = keep.tile([P, P], F32)
+        ident_bf16 = keep.tile([P, P], BF16)
+        bias_rows = keep.tile([P, P], BF16)
+        bias = keep.tile([P, FEAT_TILES], F32)
+        s2 = keep.tile([P, MEM_TILES], F32)
+        half_s2 = keep.tile([P, MEM_TILES], F32)
+        a2_parts = keep.tile([P, STATE_TILES, FEAT_PASSES], F32)
+        best = keep.tile([P, STATE_TILES], F32)
+        one = keep.tile([P, 1], F32)
+        one_root = keep.tile([P, 1], F32)
+
+        nc.vector.memset(w_scales[:].bitcast(I32), 0)
+        nc.vector.memset(bias_rows[:], 0.0)
+        nc.vector.memset(one[:], 1.0)
+        nc.scalar.activation(out=one_root[:], in_=one[:], func=ACT.Sqrt)
+        make_identity(nc, ident_f32[:])
+        make_identity(nc, ident_bf16[:])
+
+        nc.scalar.dma_start(out=bias_rows[0:FEAT_TILES, :], in_=b_feat.rearrange("(a p) -> a p", p=P))
+
+        x_rows = next_state.rearrange("(p j) k -> p j k", j=STATE_TILES)
+
+        def load_states(first_tile):
+            pair = slice(first_tile, first_tile + 2)
+            nc.sync.dma_start(out=x_sb[:, pair, :], in_=x_rows[:, pair, :])
+
+        load_states(0)
+        load_states(2)
+        for quadrant in range(4):
+            nc.sync.dma_start(
+                out=w_scales[32 * quadrant : 32 * quadrant + 4, :, :].bitcast(I32),
+                in_=Wf_scales[:, 4 * quadrant : 4 * quadrant + 4, :].rearrange("g r n -> r g n").bitcast(I32),
+            )
+        nc.sync.dma_start(out=w_words[:].bitcast(I32), in_=Wf_words.rearrange("g p b -> p g b").bitcast(I32))
+        nc.sync.dma_start(out=seen_sb[:], in_=seen.rearrange("(p a) f -> p a f", a=MEM_TILES))
+        for first_tile in range(4, STATE_TILES, 2):
+            load_states(first_tile)
+
+        bias_t = psum_t.tile([P, P], BF16, tag="t")
+        nc.tensor.transpose(out=bias_t[:], in_=bias_rows[:], identity=ident_bf16[:])
+        nc.vector.tensor_copy(out=bias[:], in_=bias_t[:, 0:FEAT_TILES])
+
+        x_grouped = {}
+        fa32 = {}
+        fa_grouped = {}
+        fa_codes = {}
+        fa_scales = {}
+        run_max = {}
+
+        def transpose_states(c, jj):
+            if jj == 0:
+                x_grouped[c] = work.tile([P, IN_PASSES, CHUNK * PACK], BF16, align_bytes=64, name="x_grouped")
+            words = x_sb[:, c * CHUNK_TILES + jj, :].bitcast(F32)
+            x_t = psum_t.tile([P, IN_PASSES, WORD_PLANES, P], F32, tag="t")
+            for g in range(IN_PASSES):
+                for u in range(WORD_PLANES):
+                    first = g * (K_PASS // 2) + u
+                    nc.tensor.transpose(
+                        out=x_t[:, g, u, :],
+                        in_=words[:, first : (g + 1) * (K_PASS // 2) : WORD_PLANES],
+                        identity=ident_f32[:],
+                    )
+            grouped_words = x_grouped[c][:].bitcast(F32)[:, :, jj * P * WORD_PLANES : (jj + 1) * P * WORD_PLANES]
+            nc.vector.tensor_copy(
+                out=grouped_words.rearrange("p g (s u) -> p g s u", u=WORD_PLANES),
+                in_=x_t[:].rearrange("p g u s -> p g s u"),
+            )
+
+        def quantise_states(c):
+            nc.vector.quantize_mx(
+                out=x_codes[:, c, :, :].rearrange("p g n -> p (g n)").bitcast(FP8X4),
+                scales=x_scales[:, c, :, :].rearrange("p g n -> p (g n)"),
+                in_=x_grouped[c][:].rearrange("p g n -> p (g n)"),
+            )
+
+        def features(c):
+            fa32[c] = work.tile([P, FEAT_TILES, CHUNK], F32, name="fa32")
+            for a in range(FEAT_TILES):
+                acc = psum_mx.tile([P, CHUNK], F32, tag="mx")
+                for g in range(IN_PASSES):
+                    nc.tensor.matmul_mx(
+                        out=acc[:],
+                        lhsT=w_words[:, g, 2 * a * P : 2 * (a + 1) * P].bitcast(FP4X4),
+                        lhsT_scale=w_scales[:, g, a * P : (a + 1) * P],
+                        rhs=x_codes[:, c, g, :].bitcast(FP8X4),
+                        rhs_scale=x_scales[:, c, g, :],
+                        start=(g == 0),
+                        stop=(g == IN_PASSES - 1),
+                    )
+                nc.scalar.activation(out=fa32[c][:, a, :], in_=acc[:], func=ACT.Relu, bias=bias[:, a : a + 1])
+
+        def square_sums(c, jj):
+            cols = slice(jj * P, (jj + 1) * P)
+            for g in range(FEAT_PASSES):
+                fa_t = psum_t.tile([P, PACK, P], F32, tag="t")
+                for t in range(PACK):
+                    nc.tensor.transpose(out=fa_t[:, t, :], in_=fa32[c][:, g * PACK + t, cols], identity=ident_f32[:])
+                squares = work.tile([P, PACK * P], BF16, name="squares")
+                nc.scalar.activation(
+                    out=squares[:],
+                    in_=fa_t[:].rearrange("p t f -> p (t f)"),
+                    func=ACT.Square,
+                    accum_out=a2_parts[:, c * CHUNK_TILES + jj, g : g + 1],
+                )
+
+        def regroup_features(c, jj):
+            if jj == 0:
+                fa_grouped[c] = work.tile([P, FEAT_PASSES, CHUNK * PACK], BF16, align_bytes=64, name="fa_grouped")
+            nc.vector.tensor_copy(
+                out=fa_grouped[c][:, :, jj * P * PACK : (jj + 1) * P * PACK].rearrange("p g (s t) -> p g s t", t=PACK),
+                in_=fa32[c][:, :, jj * P : (jj + 1) * P].rearrange("p (g t) s -> p g s t", t=PACK),
+            )
+
+        def quantise_features(c):
+            fa_codes[c] = work.tile([P, FEAT_PASSES, CHUNK], U32, align_bytes=64, name="fa_codes")
+            fa_scales[c] = work.tile([P, FEAT_PASSES, CHUNK], U8, align_bytes=64, name="fa_scales")
+            nc.vector.quantize_mx(
+                out=fa_codes[c][:].rearrange("p g n -> p (g n)").bitcast(FP8X4),
+                scales=fa_scales[c][:].rearrange("p g n -> p (g n)"),
+                in_=fa_grouped[c][:].rearrange("p g n -> p (g n)"),
+            )
+
+        def nearest(c):
+            run_max[c] = work.tile([P, CHUNK], F32, name="run_max")
+            for a in range(MEM_TILES):
+                acc = psum_mx.tile([P, CHUNK], F32, tag="mx")
+                for g in range(FEAT_PASSES):
+                    nc.tensor.matmul_mx(
+                        out=acc[:],
+                        lhsT=seen_codes[:, g, a * P : (a + 1) * P].bitcast(FP8X4),
+                        lhsT_scale=seen_scales[:, g, a * P : (a + 1) * P],
+                        rhs=fa_codes[c][:, g, :].bitcast(FP8X4),
+                        rhs_scale=fa_scales[c][:, g, :],
+                        start=(g == 0),
+                        stop=(g == FEAT_PASSES - 1),
+                    )
+                if a == 0:
+                    nc.vector.tensor_scalar(
+                        out=run_max[c][:], in0=acc[:], scalar1=half_s2[:, 0:1], scalar2=None, op0=ALU.subtract
+                    )
+                else:
+                    nc.vector.scalar_tensor_tensor(
+                        out=run_max[c][:],
+                        in0=acc[:],
+                        scalar=half_s2[:, a : a + 1],
+                        in1=run_max[c][:],
+                        op0=ALU.subtract,
+                        op1=ALU.max,
+                    )
+
+        def best_of_memory(c):
+            run_t = psum_t.tile([P, CHUNK_TILES, P], F32, tag="t")
+            for jj in range(CHUNK_TILES):
+                nc.tensor.transpose(out=run_t[:, jj, :], in_=run_max[c][:, jj * P : (jj + 1) * P], identity=ident_f32[:])
+            nc.vector.tensor_reduce(
+                out=best[:, c * CHUNK_TILES : (c + 1) * CHUNK_TILES], in_=run_t[:], axis=AXIS_X, op=ALU.max
+            )
+
+        def prepare_memory():
+            for a in range(MEM_TILES):
+                seen_squares = work.tile([P, FEATURES], BF16, name="seen_squares")
+                nc.scalar.activation(
+                    out=seen_squares[:], in_=seen_sb[:, a, :], func=ACT.Square, accum_out=s2[:, a : a + 1]
+                )
+            for g in range(FEAT_PASSES):
+                for pair in range(MEM_TILES // 2):
+                    seen_t = psum_t.tile([P, 2, PACK, P], BF16, tag="t")
+                    for b in range(2):
+                        for t in range(PACK):
+                            first = g * K_PASS + t * P
+                            nc.tensor.transpose(
+                                out=seen_t[:, b, t, :],
+                                in_=seen_sb[:, 2 * pair + b, first : first + P],
+                                identity=ident_bf16[:],
+                            )
+                    nc.vector.tensor_copy(
+                        out=seen_grouped[:, g, 2 * pair * P * PACK : 2 * (pair + 1) * P * PACK].rearrange(
+                            "p (b m t) -> p b m t", b=2, t=PACK
+                        ),
+                        in_=seen_t[:].rearrange("p b t m -> p b m t"),
+                    )
+            nc.vector.tensor_scalar(out=half_s2[:], in0=s2[:], scalar1=0.5, scalar2=None, op0=ALU.mult)
+            nc.vector.quantize_mx(
+                out=seen_codes[:].rearrange("p g n -> p (g n)").bitcast(FP8X4),
+                scales=seen_scales[:].rearrange("p g n -> p (g n)"),
+                in_=seen_grouped[:].rearrange("p g n -> p (g n)"),
+            )
+
+        for jj in range(CHUNK_TILES):
+            transpose_states(0, jj)
+        quantise_states(0)
+        features(0)
+        prepare_memory()
+        for jj in range(CHUNK_TILES):
+            transpose_states(1, jj)
+        quantise_states(1)
+
+        for c in range(CHUNKS):
+            for jj in range(CHUNK_TILES):
+                if c + AHEAD < CHUNKS:
+                    transpose_states(c + AHEAD, jj)
+                square_sums(c, jj)
+                regroup_features(c, jj)
+            if c > 0:
+                best_of_memory(c - 1)
+            quantise_features(c)
+            if c + AHEAD < CHUNKS:
+                quantise_states(c + AHEAD)
+            if c + 1 < CHUNKS:
+                features(c + 1)
+            nearest(c)
+        best_of_memory(CHUNKS - 1)
+
+        a2 = keep.tile([P, STATE_TILES], F32)
+        d2 = keep.tile([P, STATE_TILES], F32)
+        dist = keep.tile([P, STATE_TILES], F32)
+        result = keep.tile([P, STATE_TILES], F32)
+        nc.vector.tensor_reduce(out=a2[:], in_=a2_parts[:], axis=AXIS_X, op=ALU.add)
+        nc.vector.scalar_tensor_tensor(out=d2[:], in0=best[:], scalar=-2.0, in1=a2[:], op0=ALU.mult, op1=ALU.add)
+        nc.vector.tensor_scalar(out=d2[:], in0=d2[:], scalar1=SQRT_FLOOR, scalar2=None, op0=ALU.max)
+        nc.scalar.activation(out=dist[:], in_=d2[:], func=ACT.Sqrt)
+        nc.vector.tensor_scalar(out=result[:], in0=dist[:], scalar1=0.1, scalar2=1.0, op0=ALU.mult, op1=ALU.min)
+        nc.sync.dma_start(out=out.rearrange("(p j) -> p j", j=STATE_TILES), in_=result[:])

@@ -32,7 +32,10 @@ CHUNK = 512
 CHUNK_TILES = CHUNK // P
 CHUNKS = STATES // CHUNK
 WORD_PLANES = 2
-AHEAD = 2
+STATES_LEAD = 2 * CHUNK_TILES
+NEAREST_LAG = 1
+TILES_PER_STEP = FEAT_TILES // CHUNK_TILES
+assert MEM_TILES == CHUNK_TILES
 SQRT_FLOOR = 1e-30
 
 FLOPS = 2 * STATES * STATE_DIM * FEATURES + 2 * STATES * FEATURES * MEMORY
@@ -90,8 +93,10 @@ def tile_curiositymodule_pa_kernel(tc, next_state, seen, Wf_words, Wf_scales, b_
                 in_=Wf_scales[:, 4 * quadrant : 4 * quadrant + 4, :].rearrange("g r n -> r g n").bitcast(I32),
             )
         nc.sync.dma_start(out=w_words[:].bitcast(I32), in_=Wf_words.rearrange("g p b -> p g b").bitcast(I32))
+        load_states(4)
+        load_states(6)
         nc.sync.dma_start(out=seen_sb[:], in_=seen.rearrange("(p a) f -> p a f", a=MEM_TILES))
-        for first_tile in range(4, STATE_TILES, 2):
+        for first_tile in range(8, STATE_TILES, 2):
             load_states(first_tile)
 
         bias_t = psum_t.tile([P, P], BF16, tag="t")
@@ -105,10 +110,11 @@ def tile_curiositymodule_pa_kernel(tc, next_state, seen, Wf_words, Wf_scales, b_
         fa_scales = {}
         run_max = {}
 
-        def transpose_states(c, jj):
+        def transpose_states(j):
+            c, jj = divmod(j, CHUNK_TILES)
             if jj == 0:
                 x_grouped[c] = work.tile([P, IN_PASSES, CHUNK * PACK], BF16, align_bytes=64, name="x_grouped")
-            words = x_sb[:, c * CHUNK_TILES + jj, :].bitcast(F32)
+            words = x_sb[:, j, :].bitcast(F32)
             x_t = psum_t.tile([P, IN_PASSES, WORD_PLANES, P], F32, tag="t")
             for g in range(IN_PASSES):
                 for u in range(WORD_PLANES):
@@ -131,80 +137,83 @@ def tile_curiositymodule_pa_kernel(tc, next_state, seen, Wf_words, Wf_scales, b_
                 in_=x_grouped[c][:].rearrange("p g n -> p (g n)"),
             )
 
-        def features(c):
-            fa32[c] = work.tile([P, FEAT_TILES, CHUNK], F32, name="fa32")
-            for a in range(FEAT_TILES):
-                acc = psum_mx.tile([P, CHUNK], F32, tag="mx")
-                for g in range(IN_PASSES):
-                    nc.tensor.matmul_mx(
-                        out=acc[:],
-                        lhsT=w_words[:, g, 2 * a * P : 2 * (a + 1) * P].bitcast(FP4X4),
-                        lhsT_scale=w_scales[:, g, a * P : (a + 1) * P],
-                        rhs=x_codes[:, c, g, :].bitcast(FP8X4),
-                        rhs_scale=x_scales[:, c, g, :],
-                        start=(g == 0),
-                        stop=(g == IN_PASSES - 1),
-                    )
-                nc.scalar.activation(out=fa32[c][:, a, :], in_=acc[:], func=ACT.Relu, bias=bias[:, a : a + 1])
+        def features(c, a):
+            if a == 0:
+                fa32[c] = work.tile([P, FEAT_TILES, CHUNK], F32, name="fa32")
+            acc = psum_mx.tile([P, CHUNK], F32, tag="mx")
+            for g in range(IN_PASSES):
+                nc.tensor.matmul_mx(
+                    out=acc[:],
+                    lhsT=w_words[:, g, 2 * a * P : 2 * (a + 1) * P].bitcast(FP4X4),
+                    lhsT_scale=w_scales[:, g, a * P : (a + 1) * P],
+                    rhs=x_codes[:, c, g, :].bitcast(FP8X4),
+                    rhs_scale=x_scales[:, c, g, :],
+                    start=(g == 0),
+                    stop=(g == IN_PASSES - 1),
+                )
+            nc.scalar.activation(out=fa32[c][:, a, :], in_=acc[:], func=ACT.Relu, bias=bias[:, a : a + 1])
 
-        def square_sums(c, jj):
-            cols = slice(jj * P, (jj + 1) * P)
+        def square_sums(j):
+            c, jj = divmod(j, CHUNK_TILES)
             for g in range(FEAT_PASSES):
                 fa_t = psum_t.tile([P, PACK, P], F32, tag="t")
                 for t in range(PACK):
-                    nc.tensor.transpose(out=fa_t[:, t, :], in_=fa32[c][:, g * PACK + t, cols], identity=ident_f32[:])
+                    nc.tensor.transpose(
+                        out=fa_t[:, t, :], in_=fa32[c][:, g * PACK + t, jj * P : (jj + 1) * P], identity=ident_f32[:]
+                    )
                 squares = work.tile([P, PACK * P], BF16, name="squares")
                 nc.scalar.activation(
                     out=squares[:],
                     in_=fa_t[:].rearrange("p t f -> p (t f)"),
                     func=ACT.Square,
-                    accum_out=a2_parts[:, c * CHUNK_TILES + jj, g : g + 1],
+                    accum_out=a2_parts[:, j, g : g + 1],
                 )
 
-        def regroup_features(c, jj):
-            if jj == 0:
+        def regroup_features(c, g):
+            if g == 0:
                 fa_grouped[c] = work.tile([P, FEAT_PASSES, CHUNK * PACK], BF16, align_bytes=64, name="fa_grouped")
-            nc.vector.tensor_copy(
-                out=fa_grouped[c][:, :, jj * P * PACK : (jj + 1) * P * PACK].rearrange("p g (s t) -> p g s t", t=PACK),
-                in_=fa32[c][:, :, jj * P : (jj + 1) * P].rearrange("p (g t) s -> p g s t", t=PACK),
-            )
+            grouped = fa_grouped[c][:, g, :].rearrange("p (s t) -> p s t", t=PACK)
+            tiles = fa32[c][:, g * PACK : (g + 1) * PACK, :].rearrange("p t s -> p s t")
+            if g < FEAT_PASSES - 1:
+                nc.gpsimd.tensor_scalar(out=grouped, in0=tiles, scalar1=1.0, scalar2=0.0, op0=ALU.mult, op1=ALU.add)
+            else:
+                nc.vector.tensor_copy(out=grouped, in_=tiles)
 
-        def quantise_features(c):
-            fa_codes[c] = work.tile([P, FEAT_PASSES, CHUNK], U32, align_bytes=64, name="fa_codes")
-            fa_scales[c] = work.tile([P, FEAT_PASSES, CHUNK], U8, align_bytes=64, name="fa_scales")
+        def quantise_features(c, g):
+            if g == 0:
+                fa_codes[c] = work.tile([P, FEAT_PASSES, CHUNK], U32, align_bytes=64, name="fa_codes")
+                fa_scales[c] = work.tile([P, FEAT_PASSES, CHUNK], U8, align_bytes=64, name="fa_scales")
             nc.vector.quantize_mx(
-                out=fa_codes[c][:].rearrange("p g n -> p (g n)").bitcast(FP8X4),
-                scales=fa_scales[c][:].rearrange("p g n -> p (g n)"),
-                in_=fa_grouped[c][:].rearrange("p g n -> p (g n)"),
+                out=fa_codes[c][:, g, :].bitcast(FP8X4), scales=fa_scales[c][:, g, :], in_=fa_grouped[c][:, g, :]
             )
 
-        def nearest(c):
-            run_max[c] = work.tile([P, CHUNK], F32, name="run_max")
-            for a in range(MEM_TILES):
-                acc = psum_mx.tile([P, CHUNK], F32, tag="mx")
-                for g in range(FEAT_PASSES):
-                    nc.tensor.matmul_mx(
-                        out=acc[:],
-                        lhsT=seen_codes[:, g, a * P : (a + 1) * P].bitcast(FP8X4),
-                        lhsT_scale=seen_scales[:, g, a * P : (a + 1) * P],
-                        rhs=fa_codes[c][:, g, :].bitcast(FP8X4),
-                        rhs_scale=fa_scales[c][:, g, :],
-                        start=(g == 0),
-                        stop=(g == FEAT_PASSES - 1),
-                    )
-                if a == 0:
-                    nc.vector.tensor_scalar(
-                        out=run_max[c][:], in0=acc[:], scalar1=half_s2[:, 0:1], scalar2=None, op0=ALU.subtract
-                    )
-                else:
-                    nc.vector.scalar_tensor_tensor(
-                        out=run_max[c][:],
-                        in0=acc[:],
-                        scalar=half_s2[:, a : a + 1],
-                        in1=run_max[c][:],
-                        op0=ALU.subtract,
-                        op1=ALU.max,
-                    )
+        def nearest(c, a):
+            if a == 0:
+                run_max[c] = work.tile([P, CHUNK], F32, name="run_max")
+            acc = psum_mx.tile([P, CHUNK], F32, tag="mx")
+            for g in range(FEAT_PASSES):
+                nc.tensor.matmul_mx(
+                    out=acc[:],
+                    lhsT=seen_codes[:, g, a * P : (a + 1) * P].bitcast(FP8X4),
+                    lhsT_scale=seen_scales[:, g, a * P : (a + 1) * P],
+                    rhs=fa_codes[c][:, g, :].bitcast(FP8X4),
+                    rhs_scale=fa_scales[c][:, g, :],
+                    start=(g == 0),
+                    stop=(g == FEAT_PASSES - 1),
+                )
+            if a == 0:
+                nc.vector.tensor_scalar(
+                    out=run_max[c][:], in0=acc[:], scalar1=half_s2[:, 0:1], scalar2=None, op0=ALU.subtract
+                )
+            else:
+                nc.vector.scalar_tensor_tensor(
+                    out=run_max[c][:],
+                    in0=acc[:],
+                    scalar=half_s2[:, a : a + 1],
+                    in1=run_max[c][:],
+                    op0=ALU.subtract,
+                    op1=ALU.max,
+                )
 
         def best_of_memory(c):
             run_t = psum_t.tile([P, CHUNK_TILES, P], F32, tag="t")
@@ -214,29 +223,29 @@ def tile_curiositymodule_pa_kernel(tc, next_state, seen, Wf_words, Wf_scales, b_
                 out=best[:, c * CHUNK_TILES : (c + 1) * CHUNK_TILES], in_=run_t[:], axis=AXIS_X, op=ALU.max
             )
 
-        def prepare_memory():
-            for a in range(MEM_TILES):
-                seen_squares = work.tile([P, FEATURES], BF16, name="seen_squares")
-                nc.scalar.activation(
-                    out=seen_squares[:], in_=seen_sb[:, a, :], func=ACT.Square, accum_out=s2[:, a : a + 1]
+        def transpose_memory(g):
+            for pair in range(MEM_TILES // 2):
+                seen_t = psum_t.tile([P, 2, PACK, P], BF16, tag="t")
+                for b in range(2):
+                    for t in range(PACK):
+                        first = g * K_PASS + t * P
+                        nc.tensor.transpose(
+                            out=seen_t[:, b, t, :],
+                            in_=seen_sb[:, 2 * pair + b, first : first + P],
+                            identity=ident_bf16[:],
+                        )
+                nc.vector.tensor_copy(
+                    out=seen_grouped[:, g, 2 * pair * P * PACK : 2 * (pair + 1) * P * PACK].rearrange(
+                        "p (b m t) -> p b m t", b=2, t=PACK
+                    ),
+                    in_=seen_t[:].rearrange("p b t m -> p b m t"),
                 )
-            for g in range(FEAT_PASSES):
-                for pair in range(MEM_TILES // 2):
-                    seen_t = psum_t.tile([P, 2, PACK, P], BF16, tag="t")
-                    for b in range(2):
-                        for t in range(PACK):
-                            first = g * K_PASS + t * P
-                            nc.tensor.transpose(
-                                out=seen_t[:, b, t, :],
-                                in_=seen_sb[:, 2 * pair + b, first : first + P],
-                                identity=ident_bf16[:],
-                            )
-                    nc.vector.tensor_copy(
-                        out=seen_grouped[:, g, 2 * pair * P * PACK : 2 * (pair + 1) * P * PACK].rearrange(
-                            "p (b m t) -> p b m t", b=2, t=PACK
-                        ),
-                        in_=seen_t[:].rearrange("p b t m -> p b m t"),
-                    )
+
+        def memory_square_sum(a):
+            seen_squares = work.tile([P, FEATURES], BF16, name="seen_squares")
+            nc.scalar.activation(out=seen_squares[:], in_=seen_sb[:, a, :], func=ACT.Square, accum_out=s2[:, a : a + 1])
+
+        def quantise_memory():
             nc.vector.tensor_scalar(out=half_s2[:], in0=s2[:], scalar1=0.5, scalar2=None, op0=ALU.mult)
             nc.vector.quantize_mx(
                 out=seen_codes[:].rearrange("p g n -> p (g n)").bitcast(FP8X4),
@@ -244,30 +253,40 @@ def tile_curiositymodule_pa_kernel(tc, next_state, seen, Wf_words, Wf_scales, b_
                 in_=seen_grouped[:].rearrange("p g n -> p (g n)"),
             )
 
-        for jj in range(CHUNK_TILES):
-            transpose_states(0, jj)
-        quantise_states(0)
-        features(0)
-        prepare_memory()
-        for jj in range(CHUNK_TILES):
-            transpose_states(1, jj)
-        quantise_states(1)
+        for step in range(-STATES_LEAD, STATE_TILES + NEAREST_LAG + 1):
+            x_tile = step + STATES_LEAD
+            feat_chunk, feat_part = divmod(step + CHUNK_TILES, CHUNK_TILES)
+            near_chunk, near_tile = divmod(step - NEAREST_LAG, MEM_TILES)
 
-        for c in range(CHUNKS):
-            for jj in range(CHUNK_TILES):
-                if c + AHEAD < CHUNKS:
-                    transpose_states(c + AHEAD, jj)
-                square_sums(c, jj)
-                regroup_features(c, jj)
-            if c > 0:
-                best_of_memory(c - 1)
-            quantise_features(c)
-            if c + AHEAD < CHUNKS:
-                quantise_states(c + AHEAD)
-            if c + 1 < CHUNKS:
-                features(c + 1)
-            nearest(c)
-        best_of_memory(CHUNKS - 1)
+            if near_tile == 0 and 1 <= near_chunk <= CHUNKS:
+                best_of_memory(near_chunk - 1)
+            if x_tile < STATE_TILES:
+                transpose_states(x_tile)
+            if -FEAT_PASSES <= step < 0:
+                transpose_memory(step + FEAT_PASSES)
+            if 0 <= step < STATE_TILES:
+                square_sums(step)
+
+            if x_tile < STATE_TILES and x_tile % CHUNK_TILES == CHUNK_TILES - 1:
+                quantise_states(x_tile // CHUNK_TILES)
+            if feat_part == CHUNK_TILES - 1 and 0 <= feat_chunk < CHUNKS:
+                quantise_features(feat_chunk, 0)
+            if feat_part == 0 and 1 <= feat_chunk <= CHUNKS:
+                quantise_features(feat_chunk - 1, 1)
+            if step == 0:
+                quantise_memory()
+
+            if 0 <= feat_chunk < CHUNKS:
+                for a in range(feat_part * TILES_PER_STEP, (feat_part + 1) * TILES_PER_STEP):
+                    features(feat_chunk, a)
+            if -FEAT_PASSES <= step < 0:
+                for a in range((step + FEAT_PASSES) * 2, (step + FEAT_PASSES) * 2 + 2):
+                    memory_square_sum(a)
+            if 0 <= near_chunk < CHUNKS:
+                nearest(near_chunk, near_tile)
+
+            if 0 <= feat_chunk < CHUNKS and (feat_part + 1) * TILES_PER_STEP % PACK == 0:
+                regroup_features(feat_chunk, (feat_part + 1) * TILES_PER_STEP // PACK - 1)
 
         a2 = keep.tile([P, STATE_TILES], F32)
         d2 = keep.tile([P, STATE_TILES], F32)

@@ -34,8 +34,11 @@ CHUNKS = STATES // CHUNK
 WORD_PLANES = 2
 STATES_LEAD = 2 * CHUNK_TILES
 NEAREST_LAG = 1
-TILES_PER_STEP = FEAT_TILES // CHUNK_TILES
-assert MEM_TILES == CHUNK_TILES
+TILES_PER_STEP = 2
+STEPS_PER_PASS = PACK // TILES_PER_STEP
+SQUARES_LAG = STEPS_PER_PASS
+NEAR_STEPS = MEM_TILES // TILES_PER_STEP
+assert FEAT_TILES == TILES_PER_STEP * CHUNK_TILES and NEAREST_LAG + NEAR_STEPS < CHUNK_TILES
 SQRT_FLOOR = 1e-30
 
 FLOPS = 2 * STATES * STATE_DIM * FEATURES + 2 * STATES * FEATURES * MEMORY
@@ -153,21 +156,19 @@ def tile_curiositymodule_pa_kernel(tc, next_state, seen, Wf_words, Wf_scales, b_
                 )
             nc.scalar.activation(out=fa32[c][:, a, :], in_=acc[:], func=ACT.Relu, bias=bias[:, a : a + 1])
 
-        def square_sums(j):
-            c, jj = divmod(j, CHUNK_TILES)
-            for g in range(FEAT_PASSES):
-                fa_t = psum_t.tile([P, PACK, P], F32, tag="t")
-                for t in range(PACK):
-                    nc.tensor.transpose(
-                        out=fa_t[:, t, :], in_=fa32[c][:, g * PACK + t, jj * P : (jj + 1) * P], identity=ident_f32[:]
-                    )
-                squares = work.tile([P, PACK * P], BF16, name="squares")
-                nc.scalar.activation(
-                    out=squares[:],
-                    in_=fa_t[:].rearrange("p t f -> p (t f)"),
-                    func=ACT.Square,
-                    accum_out=a2_parts[:, j, g : g + 1],
+        def square_sums(c, g, jj):
+            fa_t = psum_t.tile([P, PACK, P], F32, tag="t")
+            for t in range(PACK):
+                nc.tensor.transpose(
+                    out=fa_t[:, t, :], in_=fa32[c][:, g * PACK + t, jj * P : (jj + 1) * P], identity=ident_f32[:]
                 )
+            squares = work.tile([P, PACK * P], BF16, name="squares")
+            nc.scalar.activation(
+                out=squares[:],
+                in_=fa_t[:].rearrange("p t f -> p (t f)"),
+                func=ACT.Square,
+                accum_out=a2_parts[:, c * CHUNK_TILES + jj, g : g + 1],
+            )
 
         def regroup_features(c, g):
             if g == 0:
@@ -244,28 +245,31 @@ def tile_curiositymodule_pa_kernel(tc, next_state, seen, Wf_words, Wf_scales, b_
         def memory_square_sum(a):
             seen_squares = work.tile([P, FEATURES], BF16, name="seen_squares")
             nc.scalar.activation(out=seen_squares[:], in_=seen_sb[:, a, :], func=ACT.Square, accum_out=s2[:, a : a + 1])
+            nc.scalar.mul(out=half_s2[:, a : a + 1], in_=s2[:, a : a + 1], mul=0.5)
 
         def quantise_memory():
-            nc.vector.tensor_scalar(out=half_s2[:], in0=s2[:], scalar1=0.5, scalar2=None, op0=ALU.mult)
             nc.vector.quantize_mx(
                 out=seen_codes[:].rearrange("p g n -> p (g n)").bitcast(FP8X4),
                 scales=seen_scales[:].rearrange("p g n -> p (g n)"),
                 in_=seen_grouped[:].rearrange("p g n -> p (g n)"),
             )
 
-        for step in range(-STATES_LEAD, STATE_TILES + NEAREST_LAG + 1):
+        for step in range(-STATES_LEAD, STATE_TILES):
             x_tile = step + STATES_LEAD
             feat_chunk, feat_part = divmod(step + CHUNK_TILES, CHUNK_TILES)
-            near_chunk, near_tile = divmod(step - NEAREST_LAG, MEM_TILES)
+            sq_pass, sq_part = divmod(step + CHUNK_TILES - SQUARES_LAG, STEPS_PER_PASS)
+            near_chunk, near_part = divmod(step - NEAREST_LAG, CHUNK_TILES)
+            memory_step = step + FEAT_PASSES
 
-            if near_tile == 0 and 1 <= near_chunk <= CHUNKS:
-                best_of_memory(near_chunk - 1)
             if x_tile < STATE_TILES:
                 transpose_states(x_tile)
-            if -FEAT_PASSES <= step < 0:
-                transpose_memory(step + FEAT_PASSES)
-            if 0 <= step < STATE_TILES:
-                square_sums(step)
+            if 0 <= memory_step < FEAT_PASSES:
+                transpose_memory(memory_step)
+            if 0 <= sq_pass < CHUNKS * FEAT_PASSES:
+                for jj in range(sq_part * TILES_PER_STEP, (sq_part + 1) * TILES_PER_STEP):
+                    square_sums(sq_pass // FEAT_PASSES, sq_pass % FEAT_PASSES, jj)
+            if 0 <= near_chunk and near_part == NEAR_STEPS:
+                best_of_memory(near_chunk)
 
             if x_tile < STATE_TILES and x_tile % CHUNK_TILES == CHUNK_TILES - 1:
                 quantise_states(x_tile // CHUNK_TILES)
@@ -279,14 +283,14 @@ def tile_curiositymodule_pa_kernel(tc, next_state, seen, Wf_words, Wf_scales, b_
             if 0 <= feat_chunk < CHUNKS:
                 for a in range(feat_part * TILES_PER_STEP, (feat_part + 1) * TILES_PER_STEP):
                     features(feat_chunk, a)
-            if -FEAT_PASSES <= step < 0:
-                for a in range((step + FEAT_PASSES) * 2, (step + FEAT_PASSES) * 2 + 2):
-                    memory_square_sum(a)
-            if 0 <= near_chunk < CHUNKS:
-                nearest(near_chunk, near_tile)
+            if 0 <= near_chunk and near_part < NEAR_STEPS:
+                for a in range(near_part * TILES_PER_STEP, (near_part + 1) * TILES_PER_STEP):
+                    nearest(near_chunk, a)
+            if 0 <= memory_step < MEM_TILES:
+                memory_square_sum(memory_step)
 
-            if 0 <= feat_chunk < CHUNKS and (feat_part + 1) * TILES_PER_STEP % PACK == 0:
-                regroup_features(feat_chunk, (feat_part + 1) * TILES_PER_STEP // PACK - 1)
+            if 0 <= feat_chunk < CHUNKS and feat_part % STEPS_PER_PASS == STEPS_PER_PASS - 1:
+                regroup_features(feat_chunk, feat_part // STEPS_PER_PASS)
 
         a2 = keep.tile([P, STATE_TILES], F32)
         d2 = keep.tile([P, STATE_TILES], F32)

@@ -1,3 +1,4 @@
+import math
 from contextlib import ExitStack
 
 import concourse.mybir as mybir
@@ -32,13 +33,13 @@ CHUNK = 512
 CHUNK_TILES = CHUNK // P
 CHUNKS = STATES // CHUNK
 WORD_PLANES = 2
-STATES_LEAD = 2 * CHUNK_TILES
-NEAREST_LAG = 1
+ALL = slice(0, CHUNK)
+HALVES = (slice(0, CHUNK // 2), slice(CHUNK // 2, CHUNK))
 TILES_PER_STEP = 2
 STEPS_PER_PASS = PACK // TILES_PER_STEP
-SQUARES_LAG = STEPS_PER_PASS
-NEAR_STEPS = MEM_TILES // TILES_PER_STEP
-assert FEAT_TILES == TILES_PER_STEP * CHUNK_TILES and NEAREST_LAG + NEAR_STEPS < CHUNK_TILES
+STEPS_PER_CHUNK = FEAT_PASSES * STEPS_PER_PASS
+NEAREST_LAG = STEPS_PER_CHUNK + 1
+BEST_LAG = NEAREST_LAG + MEM_TILES
 SQRT_FLOOR = 1e-30
 
 FLOPS = 2 * STATES * STATE_DIM * FEATURES + 2 * STATES * FEATURES * MEMORY
@@ -66,7 +67,6 @@ def tile_curiositymodule_pa_kernel(tc, next_state, seen, Wf_words, Wf_scales, b_
         ident_bf16 = keep.tile([P, P], BF16)
         bias_rows = keep.tile([P, P], BF16)
         bias = keep.tile([P, FEAT_TILES], F32)
-        s2 = keep.tile([P, MEM_TILES], F32)
         half_s2 = keep.tile([P, MEM_TILES], F32)
         a2_parts = keep.tile([P, STATE_TILES, FEAT_PASSES], F32)
         best = keep.tile([P, STATE_TILES], F32)
@@ -84,27 +84,23 @@ def tile_curiositymodule_pa_kernel(tc, next_state, seen, Wf_words, Wf_scales, b_
 
         x_rows = next_state.rearrange("(p j) k -> p j k", j=STATE_TILES)
 
-        def load_states(first_tile):
-            pair = slice(first_tile, first_tile + 2)
-            nc.sync.dma_start(out=x_sb[:, pair, :], in_=x_rows[:, pair, :])
+        def load_states(first_tile, tiles):
+            some = slice(first_tile, first_tile + tiles)
+            nc.sync.dma_start(out=x_sb[:, some, :], in_=x_rows[:, some, :])
 
-        load_states(0)
-        load_states(2)
+        for j in range(CHUNK_TILES):
+            load_states(j, 1)
         for quadrant in range(4):
             nc.sync.dma_start(
                 out=w_scales[32 * quadrant : 32 * quadrant + 4, :, :].bitcast(I32),
                 in_=Wf_scales[:, 4 * quadrant : 4 * quadrant + 4, :].rearrange("g r n -> r g n").bitcast(I32),
             )
         nc.sync.dma_start(out=w_words[:].bitcast(I32), in_=Wf_words.rearrange("g p b -> p g b").bitcast(I32))
-        load_states(4)
-        load_states(6)
+        load_states(CHUNK_TILES, 2)
+        load_states(CHUNK_TILES + 2, 2)
         nc.sync.dma_start(out=seen_sb[:], in_=seen.rearrange("(p a) f -> p a f", a=MEM_TILES))
-        for first_tile in range(8, STATE_TILES, 2):
-            load_states(first_tile)
-
-        bias_t = psum_t.tile([P, P], BF16, tag="t")
-        nc.tensor.transpose(out=bias_t[:], in_=bias_rows[:], identity=ident_bf16[:])
-        nc.vector.tensor_copy(out=bias[:], in_=bias_t[:, 0:FEAT_TILES])
+        for first_tile in range(2 * CHUNK_TILES, STATE_TILES, 2):
+            load_states(first_tile, 2)
 
         x_grouped = {}
         fa32 = {}
@@ -113,7 +109,7 @@ def tile_curiositymodule_pa_kernel(tc, next_state, seen, Wf_words, Wf_scales, b_
         fa_scales = {}
         run_max = {}
 
-        def transpose_states(j):
+        def transpose_states(j, copy):
             c, jj = divmod(j, CHUNK_TILES)
             if jj == 0:
                 x_grouped[c] = work.tile([P, IN_PASSES, CHUNK * PACK], BF16, align_bytes=64, name="x_grouped")
@@ -128,7 +124,7 @@ def tile_curiositymodule_pa_kernel(tc, next_state, seen, Wf_words, Wf_scales, b_
                         identity=ident_f32[:],
                     )
             grouped_words = x_grouped[c][:].bitcast(F32)[:, :, jj * P * WORD_PLANES : (jj + 1) * P * WORD_PLANES]
-            nc.vector.tensor_copy(
+            copy(
                 out=grouped_words.rearrange("p g (s u) -> p g s u", u=WORD_PLANES),
                 in_=x_t[:].rearrange("p g u s -> p g s u"),
             )
@@ -139,6 +135,16 @@ def tile_curiositymodule_pa_kernel(tc, next_state, seen, Wf_words, Wf_scales, b_
                 scales=x_scales[:, c, :, :].rearrange("p g n -> p (g n)"),
                 in_=x_grouped[c][:].rearrange("p g n -> p (g n)"),
             )
+
+        def quantise_state_tile(j):
+            c, jj = divmod(j, CHUNK_TILES)
+            cols = slice(jj * P, (jj + 1) * P)
+            for g in range(IN_PASSES):
+                nc.vector.quantize_mx(
+                    out=x_codes[:, c, g, cols].bitcast(FP8X4),
+                    scales=x_scales[:, c, g, cols],
+                    in_=x_grouped[c][:, g, jj * P * PACK : (jj + 1) * P * PACK],
+                )
 
         def features(c, a):
             if a == 0:
@@ -170,135 +176,156 @@ def tile_curiositymodule_pa_kernel(tc, next_state, seen, Wf_words, Wf_scales, b_
                 accum_out=a2_parts[:, c * CHUNK_TILES + jj, g : g + 1],
             )
 
-        def regroup_features(c, g):
-            if g == 0:
+        def regroup_features(c, g, copy, cols=ALL):
+            if c not in fa_grouped:
                 fa_grouped[c] = work.tile([P, FEAT_PASSES, CHUNK * PACK], BF16, align_bytes=64, name="fa_grouped")
-            grouped = fa_grouped[c][:, g, :].rearrange("p (s t) -> p s t", t=PACK)
-            tiles = fa32[c][:, g * PACK : (g + 1) * PACK, :].rearrange("p t s -> p s t")
-            if g < FEAT_PASSES - 1:
-                nc.gpsimd.tensor_scalar(out=grouped, in0=tiles, scalar1=1.0, scalar2=0.0, op0=ALU.mult, op1=ALU.add)
-            else:
-                nc.vector.tensor_copy(out=grouped, in_=tiles)
+            copy(
+                out=fa_grouped[c][:, g, cols.start * PACK : cols.stop * PACK].rearrange("p (s t) -> p s t", t=PACK),
+                in_=fa32[c][:, g * PACK : (g + 1) * PACK, cols].rearrange("p t s -> p s t"),
+            )
 
-        def quantise_features(c, g):
-            if g == 0:
+        def quantise_features(c, g, cols=ALL):
+            if c not in fa_codes:
                 fa_codes[c] = work.tile([P, FEAT_PASSES, CHUNK], U32, align_bytes=64, name="fa_codes")
                 fa_scales[c] = work.tile([P, FEAT_PASSES, CHUNK], U8, align_bytes=64, name="fa_scales")
             nc.vector.quantize_mx(
-                out=fa_codes[c][:, g, :].bitcast(FP8X4), scales=fa_scales[c][:, g, :], in_=fa_grouped[c][:, g, :]
+                out=fa_codes[c][:, g, cols].bitcast(FP8X4),
+                scales=fa_scales[c][:, g, cols],
+                in_=fa_grouped[c][:, g, cols.start * PACK : cols.stop * PACK],
             )
 
-        def nearest(c, a):
-            if a == 0:
+        def nearest(c, a, cols=ALL):
+            if c not in run_max:
                 run_max[c] = work.tile([P, CHUNK], F32, name="run_max")
-            acc = psum_mx.tile([P, CHUNK], F32, tag="mx")
+            acc = psum_mx.tile([P, cols.stop - cols.start], F32, tag="mx")
             for g in range(FEAT_PASSES):
                 nc.tensor.matmul_mx(
                     out=acc[:],
                     lhsT=seen_codes[:, g, a * P : (a + 1) * P].bitcast(FP8X4),
                     lhsT_scale=seen_scales[:, g, a * P : (a + 1) * P],
-                    rhs=fa_codes[c][:, g, :].bitcast(FP8X4),
-                    rhs_scale=fa_scales[c][:, g, :],
+                    rhs=fa_codes[c][:, g, cols].bitcast(FP8X4),
+                    rhs_scale=fa_scales[c][:, g, cols],
                     start=(g == 0),
                     stop=(g == FEAT_PASSES - 1),
                 )
             if a == 0:
                 nc.vector.tensor_scalar(
-                    out=run_max[c][:], in0=acc[:], scalar1=half_s2[:, 0:1], scalar2=None, op0=ALU.subtract
+                    out=run_max[c][:, cols], in0=acc[:], scalar1=half_s2[:, 0:1], scalar2=None, op0=ALU.subtract
                 )
             else:
                 nc.vector.scalar_tensor_tensor(
-                    out=run_max[c][:],
+                    out=run_max[c][:, cols],
                     in0=acc[:],
                     scalar=half_s2[:, a : a + 1],
-                    in1=run_max[c][:],
+                    in1=run_max[c][:, cols],
                     op0=ALU.subtract,
                     op1=ALU.max,
                 )
 
-        def best_of_memory(c):
-            run_t = psum_t.tile([P, CHUNK_TILES, P], F32, tag="t")
-            for jj in range(CHUNK_TILES):
-                nc.tensor.transpose(out=run_t[:, jj, :], in_=run_max[c][:, jj * P : (jj + 1) * P], identity=ident_f32[:])
-            nc.vector.tensor_reduce(
-                out=best[:, c * CHUNK_TILES : (c + 1) * CHUNK_TILES], in_=run_t[:], axis=AXIS_X, op=ALU.max
-            )
+        def best_of_memory(c, cols=ALL):
+            tiles = range(cols.start // P, cols.stop // P)
+            run_t = psum_t.tile([P, len(tiles), P], F32, tag="t")
+            for i, jj in enumerate(tiles):
+                nc.tensor.transpose(out=run_t[:, i, :], in_=run_max[c][:, jj * P : (jj + 1) * P], identity=ident_f32[:])
+            first = c * CHUNK_TILES + tiles[0]
+            nc.vector.tensor_reduce(out=best[:, first : first + len(tiles)], in_=run_t[:], axis=AXIS_X, op=ALU.max)
 
-        def transpose_memory(g):
-            for pair in range(MEM_TILES // 2):
-                seen_t = psum_t.tile([P, 2, PACK, P], BF16, tag="t")
-                for b in range(2):
-                    for t in range(PACK):
-                        first = g * K_PASS + t * P
-                        nc.tensor.transpose(
-                            out=seen_t[:, b, t, :],
-                            in_=seen_sb[:, 2 * pair + b, first : first + P],
-                            identity=ident_bf16[:],
-                        )
-                nc.vector.tensor_copy(
-                    out=seen_grouped[:, g, 2 * pair * P * PACK : 2 * (pair + 1) * P * PACK].rearrange(
-                        "p (b m t) -> p b m t", b=2, t=PACK
-                    ),
-                    in_=seen_t[:].rearrange("p b t m -> p b m t"),
-                )
+        def transpose_memory(g, pair):
+            seen_t = psum_t.tile([P, 2, PACK, P], BF16, tag="t")
+            for b in range(2):
+                for t in range(PACK):
+                    first = g * K_PASS + t * P
+                    nc.tensor.transpose(
+                        out=seen_t[:, b, t, :],
+                        in_=seen_sb[:, 2 * pair + b, first : first + P],
+                        identity=ident_bf16[:],
+                    )
+            nc.vector.tensor_copy(
+                out=seen_grouped[:, g, 2 * pair * P * PACK : 2 * (pair + 1) * P * PACK].rearrange(
+                    "p (b m t) -> p b m t", b=2, t=PACK
+                ),
+                in_=seen_t[:].rearrange("p b t m -> p b m t"),
+            )
 
         def memory_square_sum(a):
             seen_squares = work.tile([P, FEATURES], BF16, name="seen_squares")
-            nc.scalar.activation(out=seen_squares[:], in_=seen_sb[:, a, :], func=ACT.Square, accum_out=s2[:, a : a + 1])
-            nc.scalar.mul(out=half_s2[:, a : a + 1], in_=s2[:, a : a + 1], mul=0.5)
-
-        def quantise_memory():
-            nc.vector.quantize_mx(
-                out=seen_codes[:].rearrange("p g n -> p (g n)").bitcast(FP8X4),
-                scales=seen_scales[:].rearrange("p g n -> p (g n)"),
-                in_=seen_grouped[:].rearrange("p g n -> p (g n)"),
+            nc.scalar.activation(
+                out=seen_squares[:], in_=seen_sb[:, a, :], func=ACT.Square, scale=math.sqrt(0.5), accum_out=half_s2[:, a : a + 1]
             )
 
-        for step in range(-STATES_LEAD, STATE_TILES):
-            x_tile = step + STATES_LEAD
-            feat_chunk, feat_part = divmod(step + CHUNK_TILES, CHUNK_TILES)
-            sq_pass, sq_part = divmod(step + CHUNK_TILES - SQUARES_LAG, STEPS_PER_PASS)
-            near_chunk, near_part = divmod(step - NEAREST_LAG, CHUNK_TILES)
-            memory_step = step + FEAT_PASSES
+        def quantise_memory(g):
+            nc.vector.quantize_mx(out=seen_codes[:, g, :].bitcast(FP8X4), scales=seen_scales[:, g, :], in_=seen_grouped[:, g, :])
+
+        def gpsimd_copy(out, in_):
+            nc.gpsimd.tensor_scalar(out=out, in0=in_, scalar1=1.0, scalar2=0.0, op0=ALU.mult, op1=ALU.add)
+
+        for j in range(CHUNK_TILES):
+            transpose_states(j, nc.vector.tensor_copy if j % 2 == 0 else nc.scalar.copy)
+            quantise_state_tile(j)
+        bias_t = psum_t.tile([P, P], BF16, tag="t")
+        nc.tensor.transpose(out=bias_t[:], in_=bias_rows[:], identity=ident_bf16[:])
+        nc.vector.tensor_copy(out=bias[:], in_=bias_t[:, 0:FEAT_TILES])
+
+        last = CHUNKS - 1
+        for step in range(CHUNKS * STEPS_PER_CHUNK):
+            chunk, part = divmod(step, STEPS_PER_CHUNK)
+            x_tile = step + CHUNK_TILES
+            sq_pass, sq_part = divmod(step - 3, STEPS_PER_PASS)
+            rg_pass, rg_part = divmod(step - STEPS_PER_PASS, STEPS_PER_PASS)
+            near_chunk, near_tile = divmod(step - NEAREST_LAG, MEM_TILES)
+            best_chunk, best_part = divmod(step - BEST_LAG, STEPS_PER_CHUNK)
 
             if x_tile < STATE_TILES:
-                transpose_states(x_tile)
-            if 0 <= memory_step < FEAT_PASSES:
-                transpose_memory(memory_step)
-            if 0 <= sq_pass < CHUNKS * FEAT_PASSES:
+                transpose_states(x_tile, nc.vector.tensor_copy)
+            if 1 <= step <= 2 * FEAT_PASSES:
+                transpose_memory(*divmod(step - 1, 2))
+            if rg_pass >= 0 and rg_part == 0:
+                regroup_features(rg_pass // FEAT_PASSES, rg_pass % FEAT_PASSES, gpsimd_copy if rg_pass % FEAT_PASSES == 0 else nc.vector.tensor_copy)
+            if sq_pass >= 0:
                 for jj in range(sq_part * TILES_PER_STEP, (sq_part + 1) * TILES_PER_STEP):
                     square_sums(sq_pass // FEAT_PASSES, sq_pass % FEAT_PASSES, jj)
-            if 0 <= near_chunk and near_part == NEAR_STEPS:
-                best_of_memory(near_chunk)
+            if best_chunk >= 0 and best_part == 0:
+                best_of_memory(best_chunk)
+            if x_tile < STATE_TILES:
+                quantise_state_tile(x_tile)
+            if rg_pass >= 0 and rg_pass % 2 == 1 and rg_part == 0:
+                quantise_features(rg_pass // FEAT_PASSES, 1)
+            if rg_pass >= 0 and rg_pass % 2 == 0 and rg_part == 1:
+                quantise_features(rg_pass // FEAT_PASSES, 0)
+            if step in (3, 5):
+                quantise_memory((step - 3) // 2)
 
-            if x_tile < STATE_TILES and x_tile % CHUNK_TILES == CHUNK_TILES - 1:
-                quantise_states(x_tile // CHUNK_TILES)
-            if feat_part == CHUNK_TILES - 1 and 0 <= feat_chunk < CHUNKS:
-                quantise_features(feat_chunk, 0)
-            if feat_part == 0 and 1 <= feat_chunk <= CHUNKS:
-                quantise_features(feat_chunk - 1, 1)
-            if step == 0:
-                quantise_memory()
+            for a in range(part * TILES_PER_STEP, (part + 1) * TILES_PER_STEP):
+                features(chunk, a)
+            if near_chunk >= 0:
+                nearest(near_chunk, near_tile)
+            if step == 1:
+                memory_square_sum(0)
+            if step in (2, 4, 6):
+                memory_square_sum(step // 2)
 
-            if 0 <= feat_chunk < CHUNKS:
-                for a in range(feat_part * TILES_PER_STEP, (feat_part + 1) * TILES_PER_STEP):
-                    features(feat_chunk, a)
-            if 0 <= near_chunk and near_part < NEAR_STEPS:
-                for a in range(near_part * TILES_PER_STEP, (near_part + 1) * TILES_PER_STEP):
-                    nearest(near_chunk, a)
-            if 0 <= memory_step < MEM_TILES:
-                memory_square_sum(memory_step)
-
-            if 0 <= feat_chunk < CHUNKS and feat_part % STEPS_PER_PASS == STEPS_PER_PASS - 1:
-                regroup_features(feat_chunk, feat_part // STEPS_PER_PASS)
+        regroup_features(last, 1, nc.vector.tensor_copy, HALVES[0])
+        regroup_features(last, 1, gpsimd_copy, HALVES[1])
+        for cols in HALVES:
+            quantise_features(last, 1, cols)
+        for jj in range(2, CHUNK_TILES):
+            square_sums(last, 0, jj)
+        for jj in range(CHUNK_TILES):
+            square_sums(last, 1, jj)
+        nearest(last - 1, MEM_TILES - 1)
+        for cols in HALVES:
+            for a in range(MEM_TILES):
+                nearest(last, a, cols)
+        best_of_memory(last - 1)
+        for cols in HALVES:
+            best_of_memory(last, cols)
 
         a2 = keep.tile([P, STATE_TILES], F32)
         d2 = keep.tile([P, STATE_TILES], F32)
-        dist = keep.tile([P, STATE_TILES], F32)
+        clamped = keep.tile([P, STATE_TILES], F32)
         result = keep.tile([P, STATE_TILES], F32)
         nc.vector.tensor_reduce(out=a2[:], in_=a2_parts[:], axis=AXIS_X, op=ALU.add)
         nc.vector.scalar_tensor_tensor(out=d2[:], in0=best[:], scalar=-2.0, in1=a2[:], op0=ALU.mult, op1=ALU.add)
-        nc.vector.tensor_scalar(out=d2[:], in0=d2[:], scalar1=SQRT_FLOOR, scalar2=None, op0=ALU.max)
-        nc.scalar.activation(out=dist[:], in_=d2[:], func=ACT.Sqrt)
-        nc.vector.tensor_scalar(out=result[:], in0=dist[:], scalar1=0.1, scalar2=1.0, op0=ALU.mult, op1=ALU.min)
+        nc.vector.tensor_scalar(out=clamped[:], in0=d2[:], scalar1=SQRT_FLOOR, scalar2=100.0, op0=ALU.max, op1=ALU.min)
+        nc.scalar.activation(out=result[:], in_=clamped[:], func=ACT.Sqrt, scale=0.01)
         nc.sync.dma_start(out=out.rearrange("(p j) -> p j", j=STATE_TILES), in_=result[:])

@@ -96,8 +96,8 @@ def tile_curiositymodule_pa_kernel(tc, next_state, seen, Wf_words, Wf_scales, b_
                 in_=Wf_scales[:, 4 * quadrant : 4 * quadrant + 4, :].rearrange("g r n -> r g n").bitcast(I32),
             )
         nc.sync.dma_start(out=w_words[:].bitcast(I32), in_=Wf_words.rearrange("g p b -> p g b").bitcast(I32))
-        load_states(CHUNK_TILES, 2)
-        load_states(CHUNK_TILES + 2, 2)
+        for j in range(CHUNK_TILES, 2 * CHUNK_TILES):
+            load_states(j, 1)
         nc.sync.dma_start(out=seen_sb[:], in_=seen.rearrange("(p a) f -> p a f", a=MEM_TILES))
         for first_tile in range(2 * CHUNK_TILES, STATE_TILES, 2):
             load_states(first_tile, 2)
@@ -261,7 +261,10 @@ def tile_curiositymodule_pa_kernel(tc, next_state, seen, Wf_words, Wf_scales, b_
 
         for j in range(CHUNK_TILES):
             transpose_states(j, nc.vector.tensor_copy if j % 2 == 0 else nc.scalar.copy)
-            quantise_state_tile(j)
+            if j == 0 or j == 2:
+                quantise_state_tile(j // 2)
+        quantise_state_tile(2)
+        quantise_state_tile(3)
         bias_t = psum_t.tile([P, P], BF16, tag="t")
         nc.tensor.transpose(out=bias_t[:], in_=bias_rows[:], identity=ident_bf16[:])
         nc.vector.tensor_copy(out=bias[:], in_=bias_t[:, 0:FEAT_TILES])
@@ -280,7 +283,7 @@ def tile_curiositymodule_pa_kernel(tc, next_state, seen, Wf_words, Wf_scales, b_
             if 1 <= step <= 2 * FEAT_PASSES:
                 transpose_memory(*divmod(step - 1, 2))
             if rg_pass >= 0 and rg_part == 0:
-                regroup_features(rg_pass // FEAT_PASSES, rg_pass % FEAT_PASSES, gpsimd_copy if rg_pass % FEAT_PASSES == 0 else nc.vector.tensor_copy)
+                regroup_features(rg_pass // FEAT_PASSES, rg_pass % FEAT_PASSES, nc.vector.tensor_copy)
             if sq_pass >= 0:
                 for jj in range(sq_part * TILES_PER_STEP, (sq_part + 1) * TILES_PER_STEP):
                     square_sums(sq_pass // FEAT_PASSES, sq_pass % FEAT_PASSES, jj)
@@ -290,7 +293,7 @@ def tile_curiositymodule_pa_kernel(tc, next_state, seen, Wf_words, Wf_scales, b_
                 quantise_state_tile(x_tile)
             if rg_pass >= 0 and rg_pass % 2 == 1 and rg_part == 0:
                 quantise_features(rg_pass // FEAT_PASSES, 1)
-            if rg_pass >= 0 and rg_pass % 2 == 0 and rg_part == 1:
+            if rg_pass >= 0 and rg_pass % 2 == 0 and rg_part == 0:
                 quantise_features(rg_pass // FEAT_PASSES, 0)
             if step in (3, 5):
                 quantise_memory((step - 3) // 2)
@@ -310,12 +313,14 @@ def tile_curiositymodule_pa_kernel(tc, next_state, seen, Wf_words, Wf_scales, b_
             quantise_features(last, 1, cols)
         for jj in range(2, CHUNK_TILES):
             square_sums(last, 0, jj)
-        for jj in range(CHUNK_TILES):
-            square_sums(last, 1, jj)
         nearest(last - 1, MEM_TILES - 1)
-        for cols in HALVES:
-            for a in range(MEM_TILES):
+        for jj in range(2):
+            square_sums(last, 1, jj)
+        for a in range(MEM_TILES):
+            for cols in HALVES:
                 nearest(last, a, cols)
+        for jj in range(2, CHUNK_TILES):
+            square_sums(last, 1, jj)
         best_of_memory(last - 1)
         for cols in HALVES:
             best_of_memory(last, cols)

@@ -96,18 +96,32 @@ def tile_curiositymodule_pa_kernel(tc, next_state, seen, Wf_words, Wf_scales, b_
                 in_=Wf_scales[:, 4 * quadrant : 4 * quadrant + 4, :].rearrange("g r n -> r g n").bitcast(I32),
             )
         nc.sync.dma_start(out=w_words[:].bitcast(I32), in_=Wf_words.rearrange("g p b -> p g b").bitcast(I32))
-        for j in range(CHUNK_TILES, 2 * CHUNK_TILES):
+        def load_memory(pair):
+            some = slice(2 * pair, 2 * pair + 2)
+            nc.sync.dma_start(out=seen_sb[:, some, :], in_=seen.rearrange("(p a) f -> p a f", a=MEM_TILES)[:, some, :])
+
+        for j in range(CHUNK_TILES, 2 * CHUNK_TILES - 1):
             load_states(j, 1)
-        nc.sync.dma_start(out=seen_sb[:], in_=seen.rearrange("(p a) f -> p a f", a=MEM_TILES))
+        load_memory(0)
+        load_states(2 * CHUNK_TILES - 1, 1)
+        load_memory(1)
         for first_tile in range(2 * CHUNK_TILES, STATE_TILES, 2):
             load_states(first_tile, 2)
 
         x_grouped = {}
+        by_plane = {}
         fa32 = {}
         fa_grouped = {}
         fa_codes = {}
         fa_scales = {}
         run_max = {}
+
+        def part_words(j, copy):
+            by_plane[j] = work.tile([P, IN_PASSES, WORD_PLANES, P], F32, name="by_plane", bufs=3)
+            copy(
+                out=by_plane[j][:],
+                in_=x_sb[:, j, :].bitcast(F32).rearrange("p (g k u) -> p g u k", g=IN_PASSES, u=WORD_PLANES),
+            )
 
         def transpose_states(j, copy):
             c, jj = divmod(j, CHUNK_TILES)
@@ -120,7 +134,7 @@ def tile_curiositymodule_pa_kernel(tc, next_state, seen, Wf_words, Wf_scales, b_
                     first = g * (K_PASS // 2) + u
                     nc.tensor.transpose(
                         out=x_t[:, g, u, :],
-                        in_=words[:, first : (g + 1) * (K_PASS // 2) : WORD_PLANES],
+                        in_=by_plane[j][:, g, u, :] if j in by_plane else words[:, first : (g + 1) * (K_PASS // 2) : WORD_PLANES],
                         identity=ident_f32[:],
                     )
             grouped_words = x_grouped[c][:].bitcast(F32)[:, :, jj * P * WORD_PLANES : (jj + 1) * P * WORD_PLANES]
@@ -136,14 +150,14 @@ def tile_curiositymodule_pa_kernel(tc, next_state, seen, Wf_words, Wf_scales, b_
                 in_=x_grouped[c][:].rearrange("p g n -> p (g n)"),
             )
 
-        def quantise_state_tile(j):
+        def quantise_state_tiles(j, tiles):
             c, jj = divmod(j, CHUNK_TILES)
-            cols = slice(jj * P, (jj + 1) * P)
+            cols = slice(jj * P, (jj + tiles) * P)
             for g in range(IN_PASSES):
                 nc.vector.quantize_mx(
                     out=x_codes[:, c, g, cols].bitcast(FP8X4),
                     scales=x_scales[:, c, g, cols],
-                    in_=x_grouped[c][:, g, jj * P * PACK : (jj + 1) * P * PACK],
+                    in_=x_grouped[c][:, g, cols.start * PACK : cols.stop * PACK],
                 )
 
         def features(c, a):
@@ -253,18 +267,24 @@ def tile_curiositymodule_pa_kernel(tc, next_state, seen, Wf_words, Wf_scales, b_
                 out=seen_squares[:], in_=seen_sb[:, a, :], func=ACT.Square, scale=math.sqrt(0.5), accum_out=half_s2[:, a : a + 1]
             )
 
-        def quantise_memory(g):
-            nc.vector.quantize_mx(out=seen_codes[:, g, :].bitcast(FP8X4), scales=seen_scales[:, g, :], in_=seen_grouped[:, g, :])
+        def quantise_memory(pair):
+            cols = slice(2 * pair * P, 2 * (pair + 1) * P)
+            for g in range(FEAT_PASSES):
+                nc.vector.quantize_mx(
+                    out=seen_codes[:, g, cols].bitcast(FP8X4),
+                    scales=seen_scales[:, g, cols],
+                    in_=seen_grouped[:, g, cols.start * PACK : cols.stop * PACK],
+                )
 
         def gpsimd_copy(out, in_):
             nc.gpsimd.tensor_scalar(out=out, in0=in_, scalar1=1.0, scalar2=0.0, op0=ALU.mult, op1=ALU.add)
 
         for j in range(CHUNK_TILES):
             transpose_states(j, nc.vector.tensor_copy if j % 2 == 0 else nc.scalar.copy)
-            if j == 0 or j == 2:
-                quantise_state_tile(j // 2)
-        quantise_state_tile(2)
-        quantise_state_tile(3)
+            if j % 2 == 0:
+                quantise_state_tiles(j // 2, 1)
+        for j in range(CHUNK_TILES // 2, CHUNK_TILES):
+            quantise_state_tiles(j, 1)
         bias_t = psum_t.tile([P, P], BF16, tag="t")
         nc.tensor.transpose(out=bias_t[:], in_=bias_rows[:], identity=ident_bf16[:])
         nc.vector.tensor_copy(out=bias[:], in_=bias_t[:, 0:FEAT_TILES])
@@ -277,49 +297,50 @@ def tile_curiositymodule_pa_kernel(tc, next_state, seen, Wf_words, Wf_scales, b_
             rg_pass, rg_part = divmod(step - STEPS_PER_PASS, STEPS_PER_PASS)
             near_chunk, near_tile = divmod(step - NEAREST_LAG, MEM_TILES)
             best_chunk, best_part = divmod(step - BEST_LAG, STEPS_PER_CHUNK)
+            memory_part = step - 2
 
+            if memory_part in (2, 4):
+                quantise_memory(memory_part // 2 - 1)
             if x_tile < STATE_TILES:
                 transpose_states(x_tile, nc.vector.tensor_copy)
-            if 1 <= step <= 2 * FEAT_PASSES:
-                transpose_memory(*divmod(step - 1, 2))
+            if 0 <= memory_part < 2 * FEAT_PASSES:
+                transpose_memory(memory_part % 2, memory_part // 2)
             if rg_pass >= 0 and rg_part == 0:
-                regroup_features(rg_pass // FEAT_PASSES, rg_pass % FEAT_PASSES, nc.vector.tensor_copy)
+                regroup_features(rg_pass // FEAT_PASSES, rg_pass % FEAT_PASSES, gpsimd_copy if rg_pass % FEAT_PASSES == 0 else nc.vector.tensor_copy)
             if sq_pass >= 0:
                 for jj in range(sq_part * TILES_PER_STEP, (sq_part + 1) * TILES_PER_STEP):
                     square_sums(sq_pass // FEAT_PASSES, sq_pass % FEAT_PASSES, jj)
             if best_chunk >= 0 and best_part == 0:
                 best_of_memory(best_chunk)
-            if x_tile < STATE_TILES:
-                quantise_state_tile(x_tile)
-            if rg_pass >= 0 and rg_pass % 2 == 1 and rg_part == 0:
-                quantise_features(rg_pass // FEAT_PASSES, 1)
-            if rg_pass >= 0 and rg_pass % 2 == 0 and rg_part == 0:
-                quantise_features(rg_pass // FEAT_PASSES, 0)
-            if step in (3, 5):
-                quantise_memory((step - 3) // 2)
+            if x_tile < STATE_TILES and x_tile % 2 == 1:
+                quantise_state_tiles(x_tile - 1, 2)
+            if x_tile + 2 < STATE_TILES:
+                part_words(x_tile + 2, nc.vector.tensor_copy)
+            if rg_pass >= 0 and rg_part == 1 - rg_pass % FEAT_PASSES:
+                quantise_features(rg_pass // FEAT_PASSES, rg_pass % FEAT_PASSES)
 
             for a in range(part * TILES_PER_STEP, (part + 1) * TILES_PER_STEP):
                 features(chunk, a)
             if near_chunk >= 0:
                 nearest(near_chunk, near_tile)
-            if step == 1:
-                memory_square_sum(0)
-            if step in (2, 4, 6):
-                memory_square_sum(step // 2)
+            for a in range(MEM_TILES):
+                if step == [2,3,5,6][a]:
+                    memory_square_sum(a)
 
-        regroup_features(last, 1, nc.vector.tensor_copy, HALVES[0])
-        regroup_features(last, 1, gpsimd_copy, HALVES[1])
+        thirds = (slice(0, CHUNK // 2), slice(CHUNK // 2, 3 * CHUNK // 4), slice(3 * CHUNK // 4, CHUNK))
+        for cols in HALVES:
+            regroup_features(last, 1, nc.vector.tensor_copy, cols)
         for cols in HALVES:
             quantise_features(last, 1, cols)
         for jj in range(2, CHUNK_TILES):
             square_sums(last, 0, jj)
         nearest(last - 1, MEM_TILES - 1)
-        for jj in range(2):
+        for jj in range(4):
             square_sums(last, 1, jj)
         for a in range(MEM_TILES):
             for cols in HALVES:
                 nearest(last, a, cols)
-        for jj in range(2, CHUNK_TILES):
+        for jj in range(4, CHUNK_TILES):
             square_sums(last, 1, jj)
         best_of_memory(last - 1)
         for cols in HALVES:

@@ -109,19 +109,11 @@ def tile_curiositymodule_pa_kernel(tc, next_state, seen, Wf_words, Wf_scales, b_
             load_states(first_tile, 2)
 
         x_grouped = {}
-        by_plane = {}
         fa32 = {}
         fa_grouped = {}
         fa_codes = {}
         fa_scales = {}
         run_max = {}
-
-        def part_words(j, copy):
-            by_plane[j] = work.tile([P, IN_PASSES, WORD_PLANES, P], F32, name="by_plane", bufs=3)
-            copy(
-                out=by_plane[j][:],
-                in_=x_sb[:, j, :].bitcast(F32).rearrange("p (g k u) -> p g u k", g=IN_PASSES, u=WORD_PLANES),
-            )
 
         def transpose_states(j, copy):
             c, jj = divmod(j, CHUNK_TILES)
@@ -134,7 +126,7 @@ def tile_curiositymodule_pa_kernel(tc, next_state, seen, Wf_words, Wf_scales, b_
                     first = g * (K_PASS // 2) + u
                     nc.tensor.transpose(
                         out=x_t[:, g, u, :],
-                        in_=by_plane[j][:, g, u, :] if j in by_plane else words[:, first : (g + 1) * (K_PASS // 2) : WORD_PLANES],
+                        in_=words[:, first : (g + 1) * (K_PASS // 2) : WORD_PLANES],
                         identity=ident_f32[:],
                     )
             grouped_words = x_grouped[c][:].bitcast(F32)[:, :, jj * P * WORD_PLANES : (jj + 1) * P * WORD_PLANES]
@@ -306,7 +298,7 @@ def tile_curiositymodule_pa_kernel(tc, next_state, seen, Wf_words, Wf_scales, b_
             if 0 <= memory_part < 2 * FEAT_PASSES:
                 transpose_memory(memory_part % 2, memory_part // 2)
             if rg_pass >= 0 and rg_part == 0:
-                regroup_features(rg_pass // FEAT_PASSES, rg_pass % FEAT_PASSES, gpsimd_copy if rg_pass % FEAT_PASSES == 0 else nc.vector.tensor_copy)
+                regroup_features(rg_pass // FEAT_PASSES, rg_pass % FEAT_PASSES, nc.vector.tensor_copy)
             if sq_pass >= 0:
                 for jj in range(sq_part * TILES_PER_STEP, (sq_part + 1) * TILES_PER_STEP):
                     square_sums(sq_pass // FEAT_PASSES, sq_pass % FEAT_PASSES, jj)
@@ -314,9 +306,7 @@ def tile_curiositymodule_pa_kernel(tc, next_state, seen, Wf_words, Wf_scales, b_
                 best_of_memory(best_chunk)
             if x_tile < STATE_TILES and x_tile % 2 == 1:
                 quantise_state_tiles(x_tile - 1, 2)
-            if x_tile + 2 < STATE_TILES:
-                part_words(x_tile + 2, nc.vector.tensor_copy)
-            if rg_pass >= 0 and rg_part == 1 - rg_pass % FEAT_PASSES:
+            if rg_pass >= 0 and rg_part == 0:
                 quantise_features(rg_pass // FEAT_PASSES, rg_pass % FEAT_PASSES)
 
             for a in range(part * TILES_PER_STEP, (part + 1) * TILES_PER_STEP):

@@ -88,22 +88,23 @@ def tile_curiositymodule_pa_kernel(tc, next_state, seen, Wf_words, Wf_scales, b_
             some = slice(first_tile, first_tile + tiles)
             nc.sync.dma_start(out=x_sb[:, some, :], in_=x_rows[:, some, :])
 
-        for j in range(CHUNK_TILES):
-            load_states(j, 1)
+        def load_memory(pair):
+            some = slice(2 * pair, 2 * pair + 2)
+            nc.sync.dma_start(out=seen_sb[:, some, :], in_=seen.rearrange("(p a) f -> p a f", a=MEM_TILES)[:, some, :])
+
+        load_states(0, 1)
+        load_states(1, 1)
+        load_states(2, 1)
+        load_states(3, 1)
         for quadrant in range(4):
             nc.sync.dma_start(
                 out=w_scales[32 * quadrant : 32 * quadrant + 4, :, :].bitcast(I32),
                 in_=Wf_scales[:, 4 * quadrant : 4 * quadrant + 4, :].rearrange("g r n -> r g n").bitcast(I32),
             )
-        nc.sync.dma_start(out=w_words[:].bitcast(I32), in_=Wf_words.rearrange("g p b -> p g b").bitcast(I32))
-        def load_memory(pair):
-            some = slice(2 * pair, 2 * pair + 2)
-            nc.sync.dma_start(out=seen_sb[:, some, :], in_=seen.rearrange("(p a) f -> p a f", a=MEM_TILES)[:, some, :])
-
-        for j in range(CHUNK_TILES, 2 * CHUNK_TILES - 1):
-            load_states(j, 1)
         load_memory(0)
-        load_states(2 * CHUNK_TILES - 1, 1)
+        nc.sync.dma_start(out=w_words[:].bitcast(I32), in_=Wf_words.rearrange("g p b -> p g b").bitcast(I32))
+        load_states(4, 2)
+        load_states(6, 2)
         load_memory(1)
         for first_tile in range(2 * CHUNK_TILES, STATE_TILES, 2):
             load_states(first_tile, 2)
@@ -275,28 +276,33 @@ def tile_curiositymodule_pa_kernel(tc, next_state, seen, Wf_words, Wf_scales, b_
             transpose_states(j, nc.vector.tensor_copy if j % 2 == 0 else nc.scalar.copy)
             if j % 2 == 0:
                 quantise_state_tiles(j // 2, 1)
-        for j in range(CHUNK_TILES // 2, CHUNK_TILES):
-            quantise_state_tiles(j, 1)
         bias_t = psum_t.tile([P, P], BF16, tag="t")
         nc.tensor.transpose(out=bias_t[:], in_=bias_rows[:], identity=ident_bf16[:])
         nc.vector.tensor_copy(out=bias[:], in_=bias_t[:, 0:FEAT_TILES])
+        for j in range(CHUNK_TILES // 2, CHUNK_TILES):
+            quantise_state_tiles(j, 1)
+        for g in range(FEAT_PASSES):
+            transpose_memory(g, 0)
+        memory_square_sum(0)
 
         last = CHUNKS - 1
+        x_steps = {1:[4,5],2:[6],3:[7]}
         for step in range(CHUNKS * STEPS_PER_CHUNK):
             chunk, part = divmod(step, STEPS_PER_CHUNK)
-            x_tile = step + CHUNK_TILES
+            x_tiles = x_steps.get(step, [] if step == 0 else [step + CHUNK_TILES] if step + CHUNK_TILES < STATE_TILES else [])
             sq_pass, sq_part = divmod(step - 3, STEPS_PER_PASS)
             rg_pass, rg_part = divmod(step - STEPS_PER_PASS, STEPS_PER_PASS)
             near_chunk, near_tile = divmod(step - NEAREST_LAG, MEM_TILES)
-            best_chunk, best_part = divmod(step - BEST_LAG, STEPS_PER_CHUNK)
-            memory_part = step - 2
+            best_chunk, best_part = divmod(step - BEST_LAG - 1, STEPS_PER_CHUNK)
 
-            if memory_part in (2, 4):
-                quantise_memory(memory_part // 2 - 1)
-            if x_tile < STATE_TILES:
-                transpose_states(x_tile, nc.vector.tensor_copy)
-            if 0 <= memory_part < 2 * FEAT_PASSES:
-                transpose_memory(memory_part % 2, memory_part // 2)
+            if step == 4:
+                quantise_memory(0)
+            if step == 6:
+                quantise_memory(1)
+            for j in x_tiles:
+                transpose_states(j, nc.vector.tensor_copy)
+            for g, pair in {2:[[0,1],[1,1]]}.get(step, []):
+                transpose_memory(g, pair)
             if rg_pass >= 0 and rg_part == 0:
                 regroup_features(rg_pass // FEAT_PASSES, rg_pass % FEAT_PASSES, nc.vector.tensor_copy)
             if sq_pass >= 0:
@@ -304,8 +310,8 @@ def tile_curiositymodule_pa_kernel(tc, next_state, seen, Wf_words, Wf_scales, b_
                     square_sums(sq_pass // FEAT_PASSES, sq_pass % FEAT_PASSES, jj)
             if best_chunk >= 0 and best_part == 0:
                 best_of_memory(best_chunk)
-            if x_tile < STATE_TILES and x_tile % 2 == 1:
-                quantise_state_tiles(x_tile - 1, 2)
+            if x_tiles and x_tiles[-1] % 2 == 1:
+                quantise_state_tiles(x_tiles[-1] - 1, 2)
             if rg_pass >= 0 and rg_part == 0:
                 quantise_features(rg_pass // FEAT_PASSES, rg_pass % FEAT_PASSES)
 
@@ -314,10 +320,9 @@ def tile_curiositymodule_pa_kernel(tc, next_state, seen, Wf_words, Wf_scales, b_
             if near_chunk >= 0:
                 nearest(near_chunk, near_tile)
             for a in range(MEM_TILES):
-                if step == [2,3,5,6][a]:
+                if step == [-1,0,3,5][a]:
                     memory_square_sum(a)
 
-        thirds = (slice(0, CHUNK // 2), slice(CHUNK // 2, 3 * CHUNK // 4), slice(3 * CHUNK // 4, CHUNK))
         for cols in HALVES:
             regroup_features(last, 1, nc.vector.tensor_copy, cols)
         for cols in HALVES:

@@ -72,7 +72,9 @@ def tile_curiositymodule_pa_kernel(tc, next_state, seen, Wf_words, Wf_scales, b_
         best = keep.tile([P, STATE_TILES], F32)
         one = keep.tile([P, 1], F32)
         one_root = keep.tile([P, 1], F32)
+        warm_in = keep.tile([P, CHUNK], BF16)
 
+        nc.gpsimd.memset(warm_in[:], 0.0)
         nc.vector.memset(w_scales[:].bitcast(I32), 0)
         nc.vector.memset(bias_rows[:], 0.0)
         nc.vector.memset(one[:], 1.0)
@@ -272,6 +274,12 @@ def tile_curiositymodule_pa_kernel(tc, next_state, seen, Wf_words, Wf_scales, b_
         def gpsimd_copy(out, in_):
             nc.gpsimd.tensor_scalar(out=out, in0=in_, scalar1=1.0, scalar2=0.0, op0=ALU.mult, op1=ALU.add)
 
+        def warm_up(passes):
+            warm = psum_mx.tile([P, CHUNK], F32, tag="mx")
+            for i in range(passes):
+                nc.tensor.matmul(out=warm[:], lhsT=warm_in[:, 0:P], rhs=warm_in[:], start=True, stop=True)
+
+        warm_up(5)
         for j in range(CHUNK_TILES):
             transpose_states(j, nc.vector.tensor_copy if j % 2 == 0 else nc.scalar.copy)
             if j % 2 == 0:
@@ -281,6 +289,7 @@ def tile_curiositymodule_pa_kernel(tc, next_state, seen, Wf_words, Wf_scales, b_
         nc.vector.tensor_copy(out=bias[:], in_=bias_t[:, 0:FEAT_TILES])
         for j in range(CHUNK_TILES // 2, CHUNK_TILES):
             quantise_state_tiles(j, 1)
+        warm_up(2)
         for g in range(FEAT_PASSES):
             transpose_memory(g, 0)
         memory_square_sum(0)
@@ -301,7 +310,7 @@ def tile_curiositymodule_pa_kernel(tc, next_state, seen, Wf_words, Wf_scales, b_
                 quantise_memory(1)
             for j in x_tiles:
                 transpose_states(j, nc.vector.tensor_copy)
-            for g, pair in {2:[[0,1],[1,1]]}.get(step, []):
+            for g, pair in {2:[[0,1]],3:[[1,1]]}.get(step, []):
                 transpose_memory(g, pair)
             if rg_pass >= 0 and rg_part == 0:
                 regroup_features(rg_pass // FEAT_PASSES, rg_pass % FEAT_PASSES, nc.vector.tensor_copy)
@@ -323,8 +332,8 @@ def tile_curiositymodule_pa_kernel(tc, next_state, seen, Wf_words, Wf_scales, b_
                 if step == [-1,0,3,5][a]:
                     memory_square_sum(a)
 
-        for cols in HALVES:
-            regroup_features(last, 1, nc.vector.tensor_copy, cols)
+        regroup_features(last, 1, nc.vector.tensor_copy, HALVES[0])
+        regroup_features(last, 1, nc.vector.tensor_copy, HALVES[1])
         for cols in HALVES:
             quantise_features(last, 1, cols)
         for jj in range(2, CHUNK_TILES):
@@ -340,6 +349,7 @@ def tile_curiositymodule_pa_kernel(tc, next_state, seen, Wf_words, Wf_scales, b_
         best_of_memory(last - 1)
         for cols in HALVES:
             best_of_memory(last, cols)
+
 
         a2 = keep.tile([P, STATE_TILES], F32)
         d2 = keep.tile([P, STATE_TILES], F32)

@@ -189,8 +189,8 @@ def tile_curiositymodule_pa_kernel(tc, next_state, seen, Wf_words, Wf_scales, b_
             if c not in fa_grouped:
                 fa_grouped[c] = work.tile([P, FEAT_PASSES, CHUNK * PACK], BF16, align_bytes=64, name="fa_grouped")
             copy(
-                out=fa_grouped[c][:, g, cols.start * PACK : cols.stop * PACK].rearrange("p (s t) -> p s t", t=PACK),
-                in_=fa32[c][:, g * PACK : (g + 1) * PACK, cols].rearrange("p t s -> p s t"),
+                out=fa_grouped[c][:, g, cols.start * PACK : cols.stop * PACK].rearrange("p (s i t) -> p s t i", i=4, t=PACK),
+                in_=fa32[c][:, g * PACK : (g + 1) * PACK, cols].rearrange("p t (s i) -> p s t i", i=4),
             )
 
         def quantise_features(c, g, cols=ALL):
@@ -295,39 +295,42 @@ def tile_curiositymodule_pa_kernel(tc, next_state, seen, Wf_words, Wf_scales, b_
         memory_square_sum(0)
 
         last = CHUNKS - 1
-        x_steps = {1:[4,5],2:[6],3:[7]}
+        x_of = [[],[4,5],[6],[7],[8],[9],[10],[11],[12],[13],[14],[15],[],[],[],[]]
+        mem_of = {2:[[0,1]],3:[[1,1]]}
+        sq_of = [0,0,0,2,2,2,2,2,2,2,2,2,2,2,2,2]
+        near_of = [0,0,0,0,0,1,1,1,1,1,1,1,1,1,1,1]
+        best_at = {10:0,14:1}
+        sq_todo = [(c, g, jj) for c in range(CHUNKS) for g in range(FEAT_PASSES) for jj in range(CHUNK_TILES)]
+        near_todo = [(c, a) for c in range(CHUNKS - 1) for a in range(MEM_TILES)]
         for step in range(CHUNKS * STEPS_PER_CHUNK):
             chunk, part = divmod(step, STEPS_PER_CHUNK)
-            x_tiles = x_steps.get(step, [] if step == 0 else [step + CHUNK_TILES] if step + CHUNK_TILES < STATE_TILES else [])
-            sq_pass, sq_part = divmod(step - 3, STEPS_PER_PASS)
             rg_pass, rg_part = divmod(step - STEPS_PER_PASS, STEPS_PER_PASS)
-            near_chunk, near_tile = divmod(step - NEAREST_LAG, MEM_TILES)
-            best_chunk, best_part = divmod(step - BEST_LAG - 1, STEPS_PER_CHUNK)
-
             if step == 4:
                 quantise_memory(0)
             if step == 6:
                 quantise_memory(1)
-            for j in x_tiles:
+            for j in x_of[step]:
                 transpose_states(j, nc.vector.tensor_copy)
-            for g, pair in {2:[[0,1]],3:[[1,1]]}.get(step, []):
+            for g, pair in mem_of.get(step, []):
                 transpose_memory(g, pair)
             if rg_pass >= 0 and rg_part == 0:
                 regroup_features(rg_pass // FEAT_PASSES, rg_pass % FEAT_PASSES, nc.vector.tensor_copy)
-            if sq_pass >= 0:
-                for jj in range(sq_part * TILES_PER_STEP, (sq_part + 1) * TILES_PER_STEP):
-                    square_sums(sq_pass // FEAT_PASSES, sq_pass % FEAT_PASSES, jj)
-            if best_chunk >= 0 and best_part == 0:
-                best_of_memory(best_chunk)
-            if x_tiles and x_tiles[-1] % 2 == 1:
-                quantise_state_tiles(x_tiles[-1] - 1, 2)
+            for c, g, jj in sq_todo[: sq_of[step]]:
+                square_sums(c, g, jj)
+            sq_todo = sq_todo[sq_of[step] :]
+            if step in best_at:
+                best_of_memory(best_at[step])
+            for j in x_of[step]:
+                if j % 2 == 1:
+                    quantise_state_tiles(j - 1, 2)
             if rg_pass >= 0 and rg_part == 0:
                 quantise_features(rg_pass // FEAT_PASSES, rg_pass % FEAT_PASSES)
-
             for a in range(part * TILES_PER_STEP, (part + 1) * TILES_PER_STEP):
                 features(chunk, a)
-            if near_chunk >= 0:
-                nearest(near_chunk, near_tile)
+            near_now = near_todo[: near_of[step]]
+            near_todo = near_todo[near_of[step] :]
+            for c, a in near_now:
+                nearest(c, a)
             for a in range(MEM_TILES):
                 if step == [-1,0,3,5][a]:
                     memory_square_sum(a)
@@ -336,20 +339,20 @@ def tile_curiositymodule_pa_kernel(tc, next_state, seen, Wf_words, Wf_scales, b_
         regroup_features(last, 1, nc.vector.tensor_copy, HALVES[1])
         for cols in HALVES:
             quantise_features(last, 1, cols)
-        for jj in range(2, CHUNK_TILES):
-            square_sums(last, 0, jj)
-        nearest(last - 1, MEM_TILES - 1)
-        for jj in range(4):
-            square_sums(last, 1, jj)
+        for c, g, jj in sq_todo[:2]:
+            square_sums(c, g, jj)
+        for c, a in near_todo:
+            nearest(c, a)
+        for c, g, jj in sq_todo[2:6]:
+            square_sums(c, g, jj)
         for a in range(MEM_TILES):
             for cols in HALVES:
                 nearest(last, a, cols)
-        for jj in range(4, CHUNK_TILES):
-            square_sums(last, 1, jj)
+        for c, g, jj in sq_todo[6:]:
+            square_sums(c, g, jj)
         best_of_memory(last - 1)
         for cols in HALVES:
             best_of_memory(last, cols)
-
 
         a2 = keep.tile([P, STATE_TILES], F32)
         d2 = keep.tile([P, STATE_TILES], F32)

@@ -169,7 +169,12 @@ def tile_curiositymodule_pa_kernel(tc, next_state, seen, Wf_words, Wf_scales, b_
                     start=(g == 0),
                     stop=(g == IN_PASSES - 1),
                 )
-            nc.scalar.activation(out=fa32[c][:, a, :], in_=acc[:], func=ACT.Relu, bias=bias[:, a : a + 1])
+            if a in (7,):
+                nc.vector.tensor_scalar(
+                    out=fa32[c][:, a, :], in0=acc[:], scalar1=bias[:, a : a + 1], scalar2=0.0, op0=ALU.add, op1=ALU.max
+                )
+            else:
+                nc.scalar.activation(out=fa32[c][:, a, :], in_=acc[:], func=ACT.Relu, bias=bias[:, a : a + 1])
 
         def square_sums(c, g, jj):
             fa_t = psum_t.tile([P, PACK, P], F32, tag="t")
@@ -239,7 +244,7 @@ def tile_curiositymodule_pa_kernel(tc, next_state, seen, Wf_words, Wf_scales, b_
             first = c * CHUNK_TILES + tiles[0]
             nc.vector.tensor_reduce(out=best[:, first : first + len(tiles)], in_=run_t[:], axis=AXIS_X, op=ALU.max)
 
-        def transpose_memory(g, pair):
+        def transpose_memory(g, pair, copy=nc.vector.tensor_copy):
             seen_t = psum_t.tile([P, 2, PACK, P], BF16, tag="t")
             for b in range(2):
                 for t in range(PACK):
@@ -249,7 +254,7 @@ def tile_curiositymodule_pa_kernel(tc, next_state, seen, Wf_words, Wf_scales, b_
                         in_=seen_sb[:, 2 * pair + b, first : first + P],
                         identity=ident_bf16[:],
                     )
-            nc.vector.tensor_copy(
+            copy(
                 out=seen_grouped[:, g, 2 * pair * P * PACK : 2 * (pair + 1) * P * PACK].rearrange(
                     "p (b m t) -> p b m t", b=2, t=PACK
                 ),
@@ -299,7 +304,7 @@ def tile_curiositymodule_pa_kernel(tc, next_state, seen, Wf_words, Wf_scales, b_
         mem_of = {2:[[0,1]],3:[[1,1]]}
         sq_of = [0,0,0,2,2,2,2,2,2,2,2,2,2,2,2,2]
         near_of = [0,0,0,0,0,1,1,1,1,1,1,1,1,1,1,1]
-        best_at = {10:0,14:1}
+        best_at = {11:0,15:1}
         sq_todo = [(c, g, jj) for c in range(CHUNKS) for g in range(FEAT_PASSES) for jj in range(CHUNK_TILES)]
         near_todo = [(c, a) for c in range(CHUNKS - 1) for a in range(MEM_TILES)]
         for step in range(CHUNKS * STEPS_PER_CHUNK):
@@ -312,7 +317,7 @@ def tile_curiositymodule_pa_kernel(tc, next_state, seen, Wf_words, Wf_scales, b_
             for j in x_of[step]:
                 transpose_states(j, nc.vector.tensor_copy)
             for g, pair in mem_of.get(step, []):
-                transpose_memory(g, pair)
+                transpose_memory(g, pair, nc.scalar.copy)
             if rg_pass >= 0 and rg_part == 0:
                 regroup_features(rg_pass // FEAT_PASSES, rg_pass % FEAT_PASSES, nc.vector.tensor_copy)
             for c, g, jj in sq_todo[: sq_of[step]]:

@@ -325,11 +325,11 @@ def tile_curiositymodule_pa_kernel(tc, next_state, seen, Wf_words, Wf_scales, b_
             sq_todo = sq_todo[sq_of[step] :]
             if step in best_at:
                 best_of_memory(best_at[step])
+            if rg_pass >= 0 and rg_part == 1:
+                quantise_features(rg_pass // FEAT_PASSES, rg_pass % FEAT_PASSES)
             for j in x_of[step]:
                 if j % 2 == 1:
                     quantise_state_tiles(j - 1, 2)
-            if rg_pass >= 0 and rg_part == 0:
-                quantise_features(rg_pass // FEAT_PASSES, rg_pass % FEAT_PASSES)
             for a in range(part * TILES_PER_STEP, (part + 1) * TILES_PER_STEP):
                 features(chunk, a)
             near_now = near_todo[: near_of[step]]

@@ -169,7 +169,7 @@ def tile_curiositymodule_pa_kernel(tc, next_state, seen, Wf_words, Wf_scales, b_
                     start=(g == 0),
                     stop=(g == IN_PASSES - 1),
                 )
-            if a in (7,):
+            if a % 2 == 1:
                 nc.vector.tensor_scalar(
                     out=fa32[c][:, a, :], in0=acc[:], scalar1=bias[:, a : a + 1], scalar2=0.0, op0=ALU.add, op1=ALU.max
                 )
@@ -303,7 +303,7 @@ def tile_curiositymodule_pa_kernel(tc, next_state, seen, Wf_words, Wf_scales, b_
         x_of = [[],[4,5],[6],[7],[8],[9],[10],[11],[12],[13],[14],[15],[],[],[],[]]
         mem_of = {2:[[0,1]],3:[[1,1]]}
         sq_of = [0,0,0,2,2,2,2,2,2,2,2,2,2,2,2,2]
-        near_of = [0,0,0,0,0,1,1,1,1,1,1,1,1,1,1,1]
+        near_of = [0,0,0,0,0,0,1,1,1,1,1,1,1,1,2,2]
         best_at = {11:0,15:1}
         sq_todo = [(c, g, jj) for c in range(CHUNKS) for g in range(FEAT_PASSES) for jj in range(CHUNK_TILES)]
         near_todo = [(c, a) for c in range(CHUNKS - 1) for a in range(MEM_TILES)]
@@ -319,7 +319,7 @@ def tile_curiositymodule_pa_kernel(tc, next_state, seen, Wf_words, Wf_scales, b_
             for g, pair in mem_of.get(step, []):
                 transpose_memory(g, pair, nc.scalar.copy)
             if rg_pass >= 0 and rg_part == 0:
-                regroup_features(rg_pass // FEAT_PASSES, rg_pass % FEAT_PASSES, nc.vector.tensor_copy)
+                regroup_features(rg_pass // FEAT_PASSES, rg_pass % FEAT_PASSES, gpsimd_copy)
             for c, g, jj in sq_todo[: sq_of[step]]:
                 square_sums(c, g, jj)
             sq_todo = sq_todo[sq_of[step] :]

@@ -50,6 +50,7 @@ def tile_curiositymodule_pa_kernel(tc, next_state, seen, Wf_words, Wf_scales, b_
     with ExitStack() as ctx:
         keep = ctx.enter_context(tc.tile_pool(name="keep", bufs=1))
         work = ctx.enter_context(tc.tile_pool(name="work", bufs=2))
+        split = ctx.enter_context(tc.tile_pool(name="split", bufs=3))
         psum_t = ctx.enter_context(tc.psum_pool(name="psum_t", bufs=4))
         psum_mx = ctx.enter_context(tc.psum_pool(name="psum_mx", bufs=4))
         ctx.enter_context(tc.manual_schedule())
@@ -111,12 +112,20 @@ def tile_curiositymodule_pa_kernel(tc, next_state, seen, Wf_words, Wf_scales, b_
         for first_tile in range(2 * CHUNK_TILES, STATE_TILES, 2):
             load_states(first_tile, 2)
 
+        x_planes = {}
         x_grouped = {}
         fa32 = {}
         fa_grouped = {}
         fa_codes = {}
         fa_scales = {}
         run_max = {}
+
+        def split_words(j):
+            x_planes[j] = split.tile([P, IN_PASSES, WORD_PLANES, P], F32, name="x_planes")
+            nc.scalar.copy(
+                out=x_planes[j][:],
+                in_=x_sb[:, j, :].bitcast(F32).rearrange("p (g w u) -> p g u w", g=IN_PASSES, u=WORD_PLANES),
+            )
 
         def transpose_states(j, copy):
             c, jj = divmod(j, CHUNK_TILES)
@@ -127,9 +136,13 @@ def tile_curiositymodule_pa_kernel(tc, next_state, seen, Wf_words, Wf_scales, b_
             for g in range(IN_PASSES):
                 for u in range(WORD_PLANES):
                     first = g * (K_PASS // 2) + u
+                    if j in x_planes:
+                        plane = x_planes[j][:, g, u, :]
+                    else:
+                        plane = words[:, first : (g + 1) * (K_PASS // 2) : WORD_PLANES]
                     nc.tensor.transpose(
                         out=x_t[:, g, u, :],
-                        in_=words[:, first : (g + 1) * (K_PASS // 2) : WORD_PLANES],
+                        in_=plane,
                         identity=ident_f32[:],
                     )
             grouped_words = x_grouped[c][:].bitcast(F32)[:, :, jj * P * WORD_PLANES : (jj + 1) * P * WORD_PLANES]
@@ -299,11 +312,12 @@ def tile_curiositymodule_pa_kernel(tc, next_state, seen, Wf_words, Wf_scales, b_
             transpose_memory(g, 0)
         memory_square_sum(0)
 
+        split_of = [[6],[7],[8],[9],[10],[11],[12],[13],[14],[15],[],[],[],[],[],[]]
         last = CHUNKS - 1
         x_of = [[],[4,5],[6],[7],[8],[9],[10],[11],[12],[13],[14],[15],[],[],[],[]]
         mem_of = {2:[[0,1]],3:[[1,1]]}
         sq_of = [0,0,0,2,2,2,2,2,2,2,2,2,2,2,2,2]
-        near_of = [0,0,0,0,0,0,1,1,1,1,1,1,1,1,2,2]
+        near_of = [0,0,0,0,0,0,1,1,1,1,1,1,1,1,1,1]
         best_at = {11:0,15:1}
         sq_todo = [(c, g, jj) for c in range(CHUNKS) for g in range(FEAT_PASSES) for jj in range(CHUNK_TILES)]
         near_todo = [(c, a) for c in range(CHUNKS - 1) for a in range(MEM_TILES)]
@@ -317,7 +331,7 @@ def tile_curiositymodule_pa_kernel(tc, next_state, seen, Wf_words, Wf_scales, b_
             for j in x_of[step]:
                 transpose_states(j, nc.vector.tensor_copy)
             for g, pair in mem_of.get(step, []):
-                transpose_memory(g, pair, nc.scalar.copy)
+                transpose_memory(g, pair, nc.vector.tensor_copy)
             if rg_pass >= 0 and rg_part == 0:
                 regroup_features(rg_pass // FEAT_PASSES, rg_pass % FEAT_PASSES, gpsimd_copy)
             for c, g, jj in sq_todo[: sq_of[step]]:
@@ -332,12 +346,14 @@ def tile_curiositymodule_pa_kernel(tc, next_state, seen, Wf_words, Wf_scales, b_
                     quantise_state_tiles(j - 1, 2)
             for a in range(part * TILES_PER_STEP, (part + 1) * TILES_PER_STEP):
                 features(chunk, a)
+            for j in split_of[step]:
+                split_words(j)
             near_now = near_todo[: near_of[step]]
             near_todo = near_todo[near_of[step] :]
             for c, a in near_now:
                 nearest(c, a)
             for a in range(MEM_TILES):
-                if step == [-1,0,3,5][a]:
+                if step == [-1,0,1,2][a]:
                     memory_square_sum(a)
 
         regroup_features(last, 1, nc.vector.tensor_copy, HALVES[0])

@@ -57,13 +57,13 @@ def tile_curiositymodule_pa_kernel(tc, next_state, seen, Wf_words, Wf_scales, b_
 
         x_sb = keep.tile([P, STATE_TILES, STATE_DIM], BF16)
         seen_sb = keep.tile([P, MEM_TILES, FEATURES], BF16)
-        w_words = keep.tile([P, IN_PASSES, 2 * FEATURES], U8, align_bytes=64)
-        w_scales = keep.tile([P, IN_PASSES, FEATURES], U8, align_bytes=64)
-        x_codes = keep.tile([P, CHUNKS, IN_PASSES, CHUNK], U32, align_bytes=64)
-        x_scales = keep.tile([P, CHUNKS, IN_PASSES, CHUNK], U8, align_bytes=64)
-        seen_grouped = keep.tile([P, FEAT_PASSES, MEMORY * PACK], BF16, align_bytes=64)
-        seen_codes = keep.tile([P, FEAT_PASSES, MEMORY], U32, align_bytes=64)
-        seen_scales = keep.tile([P, FEAT_PASSES, MEMORY], U8, align_bytes=64)
+        w_words = keep.tile([P, IN_PASSES, 2 * FEATURES], U8, align_bytes=256)
+        w_scales = keep.tile([P, IN_PASSES, FEATURES], U8, align_bytes=256)
+        x_codes = keep.tile([P, CHUNKS, IN_PASSES, CHUNK], U32, align_bytes=256)
+        x_scales = keep.tile([P, CHUNKS, IN_PASSES, CHUNK], U8, align_bytes=256)
+        seen_grouped = keep.tile([P, FEAT_PASSES, MEMORY * PACK], BF16, align_bytes=256)
+        seen_codes = keep.tile([P, FEAT_PASSES, MEMORY], U32, align_bytes=256)
+        seen_scales = keep.tile([P, FEAT_PASSES, MEMORY], U8, align_bytes=256)
         ident_f32 = keep.tile([P, P], F32)
         ident_bf16 = keep.tile([P, P], BF16)
         bias_rows = keep.tile([P, P], BF16)
@@ -130,7 +130,7 @@ def tile_curiositymodule_pa_kernel(tc, next_state, seen, Wf_words, Wf_scales, b_
         def transpose_states(j, copy):
             c, jj = divmod(j, CHUNK_TILES)
             if jj == 0:
-                x_grouped[c] = work.tile([P, IN_PASSES, CHUNK * PACK], BF16, align_bytes=64, name="x_grouped")
+                x_grouped[c] = work.tile([P, IN_PASSES, CHUNK * PACK], BF16, align_bytes=256, name="x_grouped")
             words = x_sb[:, j, :].bitcast(F32)
             x_t = psum_t.tile([P, IN_PASSES, WORD_PLANES, P], F32, tag="t")
             for g in range(IN_PASSES):
@@ -205,7 +205,7 @@ def tile_curiositymodule_pa_kernel(tc, next_state, seen, Wf_words, Wf_scales, b_
 
         def regroup_features(c, g, copy, cols=ALL):
             if c not in fa_grouped:
-                fa_grouped[c] = work.tile([P, FEAT_PASSES, CHUNK * PACK], BF16, align_bytes=64, name="fa_grouped")
+                fa_grouped[c] = work.tile([P, FEAT_PASSES, CHUNK * PACK], BF16, align_bytes=256, name="fa_grouped")
             copy(
                 out=fa_grouped[c][:, g, cols.start * PACK : cols.stop * PACK].rearrange("p (s i t) -> p s t i", i=4, t=PACK),
                 in_=fa32[c][:, g * PACK : (g + 1) * PACK, cols].rearrange("p t (s i) -> p s t i", i=4),
@@ -213,8 +213,8 @@ def tile_curiositymodule_pa_kernel(tc, next_state, seen, Wf_words, Wf_scales, b_
 
         def quantise_features(c, g, cols=ALL):
             if c not in fa_codes:
-                fa_codes[c] = work.tile([P, FEAT_PASSES, CHUNK], U32, align_bytes=64, name="fa_codes")
-                fa_scales[c] = work.tile([P, FEAT_PASSES, CHUNK], U8, align_bytes=64, name="fa_scales")
+                fa_codes[c] = work.tile([P, FEAT_PASSES, CHUNK], U32, align_bytes=256, name="fa_codes")
+                fa_scales[c] = work.tile([P, FEAT_PASSES, CHUNK], U8, align_bytes=256, name="fa_scales")
             nc.vector.quantize_mx(
                 out=fa_codes[c][:, g, cols].bitcast(FP8X4),
                 scales=fa_scales[c][:, g, cols],

import math
from contextlib import ExitStack

import concourse.mybir as mybir
from concourse.masks import make_identity

F32 = mybir.dt.float32
BF16 = mybir.dt.bfloat16
I32 = mybir.dt.int32
U32 = mybir.dt.uint32
U8 = mybir.dt.uint8
FP8X4 = mybir.dt.float8_e4m3fn_x4
FP4X4 = mybir.dt.float4_e2m1fn_x4
ALU = mybir.AluOpType
ACT = mybir.ActivationFunctionType
AXIS_X = mybir.AxisListType.X

P = 128
PACK = 4
K_PASS = P * PACK

STATES = 2048
STATE_DIM = 1024
FEATURES = 1024
MEMORY = 512

IN_PASSES = STATE_DIM // K_PASS
FEAT_PASSES = FEATURES // K_PASS
FEAT_TILES = FEATURES // P
MEM_TILES = MEMORY // P
STATE_TILES = STATES // P
CHUNK = 512
CHUNK_TILES = CHUNK // P
CHUNKS = STATES // CHUNK
WORD_PLANES = 2
ALL = slice(0, CHUNK)
HALVES = (slice(0, CHUNK // 2), slice(CHUNK // 2, CHUNK))
TILES_PER_STEP = 2
STEPS_PER_PASS = PACK // TILES_PER_STEP
STEPS_PER_CHUNK = FEAT_PASSES * STEPS_PER_PASS
NEAREST_LAG = STEPS_PER_CHUNK + 1
BEST_LAG = NEAREST_LAG + MEM_TILES
SQRT_FLOOR = 1e-30

FLOPS = 2 * STATES * STATE_DIM * FEATURES + 2 * STATES * FEATURES * MEMORY


def tile_curiositymodule_pa_kernel(tc, next_state, seen, Wf_words, Wf_scales, b_feat, out):
    nc = tc.nc
    with ExitStack() as ctx:
        keep = ctx.enter_context(tc.tile_pool(name="keep", bufs=1))
        work = ctx.enter_context(tc.tile_pool(name="work", bufs=2))
        split = ctx.enter_context(tc.tile_pool(name="split", bufs=3))
        psum_t = ctx.enter_context(tc.psum_pool(name="psum_t", bufs=4))
        psum_mx = ctx.enter_context(tc.psum_pool(name="psum_mx", bufs=4))
        ctx.enter_context(tc.manual_schedule())

        x_sb = keep.tile([P, STATE_TILES, STATE_DIM], BF16)
        seen_sb = keep.tile([P, MEM_TILES, FEATURES], BF16)
        w_words = keep.tile([P, IN_PASSES, 2 * FEATURES], U8, align_bytes=256)
        w_scales = keep.tile([P, IN_PASSES, FEATURES], U8, align_bytes=256)
        x_codes = keep.tile([P, CHUNKS, IN_PASSES, CHUNK], U32, align_bytes=256)
        x_scales = keep.tile([P, CHUNKS, IN_PASSES, CHUNK], U8, align_bytes=256)
        seen_grouped = keep.tile([P, FEAT_PASSES, MEMORY * PACK], BF16, align_bytes=256)
        seen_codes = keep.tile([P, FEAT_PASSES, MEMORY], U32, align_bytes=256)
        seen_scales = keep.tile([P, FEAT_PASSES, MEMORY], U8, align_bytes=256)
        ident_f32 = keep.tile([P, P], F32)
        ident_bf16 = keep.tile([P, P], BF16)
        bias_rows = keep.tile([P, P], BF16)
        bias = keep.tile([P, FEAT_TILES], F32)
        half_s2 = keep.tile([P, MEM_TILES], F32)
        a2_parts = keep.tile([P, STATE_TILES, FEAT_PASSES], F32)
        best = keep.tile([P, STATE_TILES], F32)
        one = keep.tile([P, 1], F32)
        one_root = keep.tile([P, 1], F32)
        warm_in = keep.tile([P, CHUNK], BF16)

        nc.gpsimd.memset(warm_in[:], 0.0)
        nc.vector.memset(w_scales[:].bitcast(I32), 0)
        nc.vector.memset(bias_rows[:], 0.0)
        nc.vector.memset(one[:], 1.0)
        nc.scalar.activation(out=one_root[:], in_=one[:], func=ACT.Sqrt)
        make_identity(nc, ident_f32[:])
        make_identity(nc, ident_bf16[:])

        nc.scalar.dma_start(out=bias_rows[0:FEAT_TILES, :], in_=b_feat.rearrange("(a p) -> a p", p=P))

        x_rows = next_state.rearrange("(p j) k -> p j k", j=STATE_TILES)

        def load_states(first_tile, tiles):
            some = slice(first_tile, first_tile + tiles)
            nc.sync.dma_start(out=x_sb[:, some, :], in_=x_rows[:, some, :])

        def load_memory(pair):
            some = slice(2 * pair, 2 * pair + 2)
            nc.sync.dma_start(out=seen_sb[:, some, :], in_=seen.rearrange("(p a) f -> p a f", a=MEM_TILES)[:, some, :])

        load_states(0, 1)
        load_states(1, 1)
        load_states(2, 1)
        load_states(3, 1)
        for quadrant in range(4):
            nc.sync.dma_start(
                out=w_scales[32 * quadrant : 32 * quadrant + 4, :, :].bitcast(I32),
                in_=Wf_scales[:, 4 * quadrant : 4 * quadrant + 4, :].rearrange("g r n -> r g n").bitcast(I32),
            )
        load_memory(0)
        nc.sync.dma_start(out=w_words[:].bitcast(I32), in_=Wf_words.rearrange("g p b -> p g b").bitcast(I32))
        load_states(4, 2)
        load_states(6, 2)
        load_memory(1)
        for first_tile in range(2 * CHUNK_TILES, STATE_TILES, 2):
            load_states(first_tile, 2)

        x_planes = {}
        x_grouped = {}
        fa32 = {}
        fa_grouped = {}
        fa_codes = {}
        fa_scales = {}
        run_max = {}

        def split_words(j):
            x_planes[j] = split.tile([P, IN_PASSES, WORD_PLANES, P], F32, name="x_planes")
            nc.scalar.copy(
                out=x_planes[j][:],
                in_=x_sb[:, j, :].bitcast(F32).rearrange("p (g w u) -> p g u w", g=IN_PASSES, u=WORD_PLANES),
            )

        def transpose_states(j, copy):
            c, jj = divmod(j, CHUNK_TILES)
            if jj == 0:
                x_grouped[c] = work.tile([P, IN_PASSES, CHUNK * PACK], BF16, align_bytes=256, name="x_grouped")
            words = x_sb[:, j, :].bitcast(F32)
            x_t = psum_t.tile([P, IN_PASSES, WORD_PLANES, P], F32, tag="t")
            for g in range(IN_PASSES):
                for u in range(WORD_PLANES):
                    first = g * (K_PASS // 2) + u
                    if j in x_planes:
                        plane = x_planes[j][:, g, u, :]
                    else:
                        plane = words[:, first : (g + 1) * (K_PASS // 2) : WORD_PLANES]
                    nc.tensor.transpose(
                        out=x_t[:, g, u, :],
                        in_=plane,
                        identity=ident_f32[:],
                    )
            grouped_words = x_grouped[c][:].bitcast(F32)[:, :, jj * P * WORD_PLANES : (jj + 1) * P * WORD_PLANES]
            copy(
                out=grouped_words.rearrange("p g (s u) -> p g s u", u=WORD_PLANES),
                in_=x_t[:].rearrange("p g u s -> p g s u"),
            )

        def quantise_states(c):
            nc.vector.quantize_mx(
                out=x_codes[:, c, :, :].rearrange("p g n -> p (g n)").bitcast(FP8X4),
                scales=x_scales[:, c, :, :].rearrange("p g n -> p (g n)"),
                in_=x_grouped[c][:].rearrange("p g n -> p (g n)"),
            )

        def quantise_state_tiles(j, tiles):
            c, jj = divmod(j, CHUNK_TILES)
            cols = slice(jj * P, (jj + tiles) * P)
            for g in range(IN_PASSES):
                nc.vector.quantize_mx(
                    out=x_codes[:, c, g, cols].bitcast(FP8X4),
                    scales=x_scales[:, c, g, cols],
                    in_=x_grouped[c][:, g, cols.start * PACK : cols.stop * PACK],
                )

        def features(c, a):
            if a == 0:
                fa32[c] = work.tile([P, FEAT_TILES, CHUNK], F32, name="fa32")
            acc = psum_mx.tile([P, CHUNK], F32, tag="mx")
            for g in range(IN_PASSES):
                nc.tensor.matmul_mx(
                    out=acc[:],
                    lhsT=w_words[:, g, 2 * a * P : 2 * (a + 1) * P].bitcast(FP4X4),
                    lhsT_scale=w_scales[:, g, a * P : (a + 1) * P],
                    rhs=x_codes[:, c, g, :].bitcast(FP8X4),
                    rhs_scale=x_scales[:, c, g, :],
                    start=(g == 0),
                    stop=(g == IN_PASSES - 1),
                )
            if a % 2 == 1:
                nc.vector.tensor_scalar(
                    out=fa32[c][:, a, :], in0=acc[:], scalar1=bias[:, a : a + 1], scalar2=0.0, op0=ALU.add, op1=ALU.max
                )
            else:
                nc.scalar.activation(out=fa32[c][:, a, :], in_=acc[:], func=ACT.Relu, bias=bias[:, a : a + 1])

        def square_sums(c, g, jj):
            fa_t = psum_t.tile([P, PACK, P], F32, tag="t")
            for t in range(PACK):
                nc.tensor.transpose(
                    out=fa_t[:, t, :], in_=fa32[c][:, g * PACK + t, jj * P : (jj + 1) * P], identity=ident_f32[:]
                )
            squares = work.tile([P, PACK * P], BF16, name="squares")
            nc.scalar.activation(
                out=squares[:],
                in_=fa_t[:].rearrange("p t f -> p (t f)"),
                func=ACT.Square,
                accum_out=a2_parts[:, c * CHUNK_TILES + jj, g : g + 1],
            )

        def regroup_features(c, g, copy, cols=ALL):
            if c not in fa_grouped:
                fa_grouped[c] = work.tile([P, FEAT_PASSES, CHUNK * PACK], BF16, align_bytes=256, name="fa_grouped")
            copy(
                out=fa_grouped[c][:, g, cols.start * PACK : cols.stop * PACK].rearrange("p (s i t) -> p s t i", i=4, t=PACK),
                in_=fa32[c][:, g * PACK : (g + 1) * PACK, cols].rearrange("p t (s i) -> p s t i", i=4),
            )

        def quantise_features(c, g, cols=ALL):
            if c not in fa_codes:
                fa_codes[c] = work.tile([P, FEAT_PASSES, CHUNK], U32, align_bytes=256, name="fa_codes")
                fa_scales[c] = work.tile([P, FEAT_PASSES, CHUNK], U8, align_bytes=256, name="fa_scales")
            nc.vector.quantize_mx(
                out=fa_codes[c][:, g, cols].bitcast(FP8X4),
                scales=fa_scales[c][:, g, cols],
                in_=fa_grouped[c][:, g, cols.start * PACK : cols.stop * PACK],
            )

        def nearest(c, a, cols=ALL):
            if c not in run_max:
                run_max[c] = work.tile([P, CHUNK], F32, name="run_max")
            acc = psum_mx.tile([P, cols.stop - cols.start], F32, tag="mx")
            for g in range(FEAT_PASSES):
                nc.tensor.matmul_mx(
                    out=acc[:],
                    lhsT=seen_codes[:, g, a * P : (a + 1) * P].bitcast(FP8X4),
                    lhsT_scale=seen_scales[:, g, a * P : (a + 1) * P],
                    rhs=fa_codes[c][:, g, cols].bitcast(FP8X4),
                    rhs_scale=fa_scales[c][:, g, cols],
                    start=(g == 0),
                    stop=(g == FEAT_PASSES - 1),
                )
            if a == 0:
                nc.vector.tensor_scalar(
                    out=run_max[c][:, cols], in0=acc[:], scalar1=half_s2[:, 0:1], scalar2=None, op0=ALU.subtract
                )
            else:
                nc.vector.scalar_tensor_tensor(
                    out=run_max[c][:, cols],
                    in0=acc[:],
                    scalar=half_s2[:, a : a + 1],
                    in1=run_max[c][:, cols],
                    op0=ALU.subtract,
                    op1=ALU.max,
                )

        def best_of_memory(c, cols=ALL):
            tiles = range(cols.start // P, cols.stop // P)
            run_t = psum_t.tile([P, len(tiles), P], F32, tag="t")
            for i, jj in enumerate(tiles):
                nc.tensor.transpose(out=run_t[:, i, :], in_=run_max[c][:, jj * P : (jj + 1) * P], identity=ident_f32[:])
            first = c * CHUNK_TILES + tiles[0]
            nc.vector.tensor_reduce(out=best[:, first : first + len(tiles)], in_=run_t[:], axis=AXIS_X, op=ALU.max)

        def transpose_memory(g, pair, copy=nc.vector.tensor_copy):
            seen_t = psum_t.tile([P, 2, PACK, P], BF16, tag="t")
            for b in range(2):
                for t in range(PACK):
                    first = g * K_PASS + t * P
                    nc.tensor.transpose(
                        out=seen_t[:, b, t, :],
                        in_=seen_sb[:, 2 * pair + b, first : first + P],
                        identity=ident_bf16[:],
                    )
            copy(
                out=seen_grouped[:, g, 2 * pair * P * PACK : 2 * (pair + 1) * P * PACK].rearrange(
                    "p (b m t) -> p b m t", b=2, t=PACK
                ),
                in_=seen_t[:].rearrange("p b t m -> p b m t"),
            )

        def memory_square_sum(a):
            seen_squares = work.tile([P, FEATURES], BF16, name="seen_squares")
            nc.scalar.activation(
                out=seen_squares[:], in_=seen_sb[:, a, :], func=ACT.Square, scale=math.sqrt(0.5), accum_out=half_s2[:, a : a + 1]
            )

        def quantise_memory(pair):
            cols = slice(2 * pair * P, 2 * (pair + 1) * P)
            for g in range(FEAT_PASSES):
                nc.vector.quantize_mx(
                    out=seen_codes[:, g, cols].bitcast(FP8X4),
                    scales=seen_scales[:, g, cols],
                    in_=seen_grouped[:, g, cols.start * PACK : cols.stop * PACK],
                )

        def gpsimd_copy(out, in_):
            nc.gpsimd.tensor_scalar(out=out, in0=in_, scalar1=1.0, scalar2=0.0, op0=ALU.mult, op1=ALU.add)

        def warm_up(passes):
            warm = psum_mx.tile([P, CHUNK], F32, tag="mx")
            for i in range(passes):
                nc.tensor.matmul(out=warm[:], lhsT=warm_in[:, 0:P], rhs=warm_in[:], start=True, stop=True)

        warm_up(5)
        for j in range(CHUNK_TILES):
            transpose_states(j, nc.vector.tensor_copy if j % 2 == 0 else nc.scalar.copy)
            if j % 2 == 0:
                quantise_state_tiles(j // 2, 1)
        bias_t = psum_t.tile([P, P], BF16, tag="t")
        nc.tensor.transpose(out=bias_t[:], in_=bias_rows[:], identity=ident_bf16[:])
        nc.vector.tensor_copy(out=bias[:], in_=bias_t[:, 0:FEAT_TILES])
        for j in range(CHUNK_TILES // 2, CHUNK_TILES):
            quantise_state_tiles(j, 1)
        warm_up(2)
        for g in range(FEAT_PASSES):
            transpose_memory(g, 0)
        memory_square_sum(0)

        split_of = [[6],[7],[8],[9],[10],[11],[12],[13],[14],[15],[],[],[],[],[],[]]
        last = CHUNKS - 1
        x_of = [[],[4,5],[6],[7],[8],[9],[10],[11],[12],[13],[14],[15],[],[],[],[]]
        mem_of = {2:[[0,1]],3:[[1,1]]}
        sq_of = [0,0,0,2,2,2,2,2,2,2,2,2,2,2,2,2]
        near_of = [0,0,0,0,0,0,1,1,1,1,1,1,1,1,1,1]
        best_at = {11:0,15:1}
        sq_todo = [(c, g, jj) for c in range(CHUNKS) for g in range(FEAT_PASSES) for jj in range(CHUNK_TILES)]
        near_todo = [(c, a) for c in range(CHUNKS - 1) for a in range(MEM_TILES)]
        for step in range(CHUNKS * STEPS_PER_CHUNK):
            chunk, part = divmod(step, STEPS_PER_CHUNK)
            rg_pass, rg_part = divmod(step - STEPS_PER_PASS, STEPS_PER_PASS)
            if step == 4:
                quantise_memory(0)
            if step == 6:
                quantise_memory(1)
            for j in x_of[step]:
                transpose_states(j, nc.vector.tensor_copy)
            for g, pair in mem_of.get(step, []):
                transpose_memory(g, pair, nc.vector.tensor_copy)
            if rg_pass >= 0 and rg_part == 0:
                regroup_features(rg_pass // FEAT_PASSES, rg_pass % FEAT_PASSES, gpsimd_copy)
            for c, g, jj in sq_todo[: sq_of[step]]:
                square_sums(c, g, jj)
            sq_todo = sq_todo[sq_of[step] :]
            if step in best_at:
                best_of_memory(best_at[step])
            if rg_pass >= 0 and rg_part == 1:
                quantise_features(rg_pass // FEAT_PASSES, rg_pass % FEAT_PASSES)
            for j in x_of[step]:
                if j % 2 == 1:
                    quantise_state_tiles(j - 1, 2)
            for a in range(part * TILES_PER_STEP, (part + 1) * TILES_PER_STEP):
                features(chunk, a)
            for j in split_of[step]:
                split_words(j)
            near_now = near_todo[: near_of[step]]
            near_todo = near_todo[near_of[step] :]
            for c, a in near_now:
                nearest(c, a)
            for a in range(MEM_TILES):
                if step == [-1,0,1,2][a]:
                    memory_square_sum(a)

        regroup_features(last, 1, nc.vector.tensor_copy, HALVES[0])
        regroup_features(last, 1, nc.vector.tensor_copy, HALVES[1])
        for cols in HALVES:
            quantise_features(last, 1, cols)
        for c, g, jj in sq_todo[:2]:
            square_sums(c, g, jj)
        for c, a in near_todo:
            nearest(c, a)
        for c, g, jj in sq_todo[2:6]:
            square_sums(c, g, jj)
        for a in range(MEM_TILES):
            for cols in HALVES:
                nearest(last, a, cols)
        for c, g, jj in sq_todo[6:]:
            square_sums(c, g, jj)
        best_of_memory(last - 1)
        for cols in HALVES:
            best_of_memory(last, cols)

        a2 = keep.tile([P, STATE_TILES], F32)
        d2 = keep.tile([P, STATE_TILES], F32)
        clamped = keep.tile([P, STATE_TILES], F32)
        result = keep.tile([P, STATE_TILES], F32)
        nc.vector.tensor_reduce(out=a2[:], in_=a2_parts[:], axis=AXIS_X, op=ALU.add)
        nc.vector.scalar_tensor_tensor(out=d2[:], in0=best[:], scalar=-2.0, in1=a2[:], op0=ALU.mult, op1=ALU.add)
        nc.vector.tensor_scalar(out=clamped[:], in0=d2[:], scalar1=SQRT_FLOOR, scalar2=100.0, op0=ALU.max, op1=ALU.min)
        nc.scalar.activation(out=result[:], in_=clamped[:], func=ACT.Sqrt, scale=0.01)
        nc.sync.dma_start(out=out.rearrange("(p j) -> p j", j=STATE_TILES), in_=result[:])
